import numpy as np
import ml_dtypes


def mxq(x, axis, fmt="e4m3"):
    dtype, down = {"e4m3": (ml_dtypes.float8_e4m3fn, 7), "e5m2": (ml_dtypes.float8_e5m2, 14)}[fmt]
    v = np.moveaxis(np.asarray(x, np.float32).astype(ml_dtypes.bfloat16).astype(np.float64), axis, -1)
    blocks = v.reshape(v.shape[:-1] + (-1, 32))
    amax = np.abs(blocks).max(-1, keepdims=True)
    byte = np.maximum(np.where(amax > 0, np.frexp(amax)[1] - 1 + 127, 0) - down, 1)
    scale = np.exp2(byte - 127.0)
    codes = (blocks / scale).astype(np.float32).astype(dtype).astype(np.float64)
    return np.moveaxis((codes * scale).reshape(v.shape), -1, axis)


WIDE = False


def mx_kscale(k):
    if not WIDE:
        return np.ones(k)
    levels = np.array([10, -10, 5, -5, 0])
    a = np.random.permutation(np.resize(levels, k // 512 * 4)).reshape(k // 512, 4)
    idx = np.arange(k)
    return np.exp2(a[idx // 512, idx % 128 // 32])


BF16 = ml_dtypes.bfloat16


def bf(x):
    return np.asarray(x, np.float32).astype(BF16)


def f64(x):
    return np.asarray(x).astype(np.float64)


E2M1 = np.array([0.0, 0.5, 1.0, 1.5, 2.0, 3.0, 4.0, 6.0, -0.0, -0.5, -1.0, -1.5, -2.0, -3.0, -4.0, -6.0])


def pack_weight(w, fmt):
    k, n = w.shape
    w = f64(bf(w)).reshape(k // 32, 32, n)
    amax = np.abs(w).max(1)
    if fmt == "e4m3":
        byte = np.frexp(amax)[1] - 1 + 127 - 7
    else:
        mant, ex = np.frexp(amax / 6.0)
        byte = np.where(mant > 0.5, ex, ex - 1) + 127
    byte = np.clip(np.where(amax > 0, byte, 1), 1, 254)
    scaled = (w * np.exp2(127.0 - byte)[:, None, :]).reshape(k, n).astype(np.float32)
    by_word = np.ascontiguousarray(scaled.reshape(k // 512, 128, 4, n).transpose(0, 1, 3, 2))
    if fmt == "e4m3":
        words = by_word.astype(ml_dtypes.float8_e4m3fn).view(np.uint8)
    else:
        c = by_word.astype(ml_dtypes.float4_e2m1fn).view(np.uint8) & 0xF
        words = c[..., 0::2] | (c[..., 1::2] << 4)
    return np.ascontiguousarray(words), np.ascontiguousarray(byte.astype(np.uint8).reshape(k // 512, 16, n))


def unpack_weight(words, scales, fmt):
    g, p, n, _ = words.shape
    if fmt == "e4m3":
        vals = np.ascontiguousarray(words).view(ml_dtypes.float8_e4m3fn).astype(np.float64)
    else:
        nib = np.empty((g, p, n, 4), np.uint8)
        nib[..., 0::2] = words & 0xF
        nib[..., 1::2] = words >> 4
        vals = E2M1[nib]
    vals = vals * np.repeat(np.exp2(scales.astype(np.float64) - 127.0), 8, axis=1)[..., None]
    return vals.transpose(0, 1, 3, 2).reshape(g * 512, n)


N, D, L = 1024, 1024, 4


def setup_inputs():
    s = mx_kscale(D)
    x = bf(np.random.standard_normal((N, D)) * s)
    w1 = np.random.standard_normal((D, D)) / np.sqrt(D) / s[None, :]
    words, scales = pack_weight(np.ascontiguousarray(w1.T), "e4m3")
    return {"x": x, "W1_words": words, "W1_scales": scales}


def reference(x, W1_words, W1_scales):
    h = mxq(f64(x), 1, "e4m3") @ unpack_weight(W1_words, W1_scales, "e4m3")
    a = h * h.T
    sq = a * a
    return sq / np.sum(sq, axis=1, keepdims=True)

@@ -1,0 +1,135 @@
+from contextlib import ExitStack
+
+import concourse.mybir as mybir
+from concourse.masks import make_identity
+
+F32 = mybir.dt.float32
+BF16 = mybir.dt.bfloat16
+I32 = mybir.dt.int32
+U32 = mybir.dt.uint32
+U8 = mybir.dt.uint8
+FP8X4 = mybir.dt.float8_e4m3fn_x4
+SQUARE = mybir.ActivationFunctionType.Square
+MULT = mybir.AluOpType.mult
+ADD = mybir.AluOpType.add
+
+P = 128
+PACK = 4
+K_PASS = P * PACK
+N = 1024
+D = 1024
+PASSES = D // K_PASS
+ROW_TILES = N // P
+BANK = 512
+HALVES = N // BANK
+
+FLOPS = 2 * N * N * D
+
+
+def tile_gcn_pa_kernel(tc, x, W1_words, W1_scales, out):
+    nc = tc.nc
+    with ExitStack() as ctx:
+        keep = ctx.enter_context(tc.tile_pool(name="keep", bufs=1))
+        x_pool = ctx.enter_context(tc.tile_pool(name="x_pool", bufs=ROW_TILES))
+        stage = ctx.enter_context(tc.tile_pool(name="stage", bufs=3))
+        psum = ctx.enter_context(tc.psum_pool(name="psum", bufs=8))
+
+        identity = keep.tile([P, P], F32)
+        make_identity(nc, identity[:])
+
+        x_codes = keep.tile([P, PASSES, N], U32, align_bytes=64)
+        x_scales = keep.tile([P, PASSES, N], U8, align_bytes=64)
+        w_codes = keep.tile([P, PASSES, N], U32, align_bytes=64)
+        w_scales = keep.tile([P, PASSES, N], U8, align_bytes=64)
+        nc.vector.memset(w_scales[:].bitcast(I32), 0)
+
+        x_rows = []
+        for i in range(ROW_TILES):
+            x_tile = x_pool.tile([P, D], BF16, tag="x_tile")
+            nc.sync.dma_start(out=x_tile[:], in_=x[i * P : (i + 1) * P, :])
+            x_rows.append(x_tile)
+        for quad in range(4):
+            nc.sync.dma_start(
+                out=w_scales[32 * quad : 32 * quad + 4, :, :].bitcast(I32),
+                in_=W1_scales[:, 4 * quad : 4 * quad + 4, :].rearrange("g r n -> r g n").bitcast(I32),
+            )
+        for g in range(PASSES):
+            nc.sync.dma_start(
+                out=w_codes[:, g, :].bitcast(I32),
+                in_=W1_words[g].rearrange("p n t -> p (n t)").bitcast(I32),
+            )
+
+        for i in range(ROW_TILES):
+            rows = slice(i * P, (i + 1) * P)
+            x_words = x_rows[i][:].bitcast(F32)
+            xt = psum.tile([P, BANK], F32, tag="bank")
+            for g in range(PASSES):
+                for u in range(2):
+                    plane = 2 * g + u
+                    nc.tensor.transpose(
+                        xt[:, plane * P : (plane + 1) * P],
+                        x_words[:, 256 * g + u : 256 * (g + 1) : 2],
+                        identity[:],
+                    )
+            grouped = stage.tile([P, PASSES, P, PACK], BF16, align_bytes=64)
+            nc.scalar.copy(
+                out=grouped[:].bitcast(F32),
+                in_=xt[:].rearrange("p (g u r) -> p g r u", g=PASSES, u=2),
+            )
+            for g in range(PASSES):
+                nc.vector.quantize_mx(
+                    out=x_codes[:, g, rows].bitcast(FP8X4),
+                    scales=x_scales[:, g, rows],
+                    in_=grouped[:, g, :, :].rearrange("p r t -> p (r t)"),
+                )
+
+        for i in range(ROW_TILES):
+            rows = slice(i * P, (i + 1) * P)
+            h_bank = []
+            ht_bank = []
+            for c in range(HALVES):
+                cols = slice(c * BANK, (c + 1) * BANK)
+                h_ps = psum.tile([P, BANK], F32, tag="bank")
+                for g in range(PASSES):
+                    nc.tensor.matmul_mx(
+                        out=h_ps[:],
+                        lhsT=x_codes[:, g, rows].bitcast(FP8X4),
+                        lhsT_scale=x_scales[:, g, rows],
+                        rhs=w_codes[:, g, cols].bitcast(FP8X4),
+                        rhs_scale=w_scales[:, g, cols],
+                        start=(g == 0),
+                        stop=(g == PASSES - 1),
+                    )
+                h_bank.append(h_ps)
+            for c in range(HALVES):
+                cols = slice(c * BANK, (c + 1) * BANK)
+                ht_ps = psum.tile([P, BANK], F32, tag="bank")
+                for g in range(PASSES):
+                    nc.tensor.matmul_mx(
+                        out=ht_ps[:],
+                        lhsT=w_codes[:, g, rows].bitcast(FP8X4),
+                        lhsT_scale=w_scales[:, g, rows],
+                        rhs=x_codes[:, g, cols].bitcast(FP8X4),
+                        rhs_scale=x_scales[:, g, cols],
+                        start=(g == 0),
+                        stop=(g == PASSES - 1),
+                    )
+                ht_bank.append(ht_ps)
+
+            h_sb = stage.tile([P, N], F32)
+            nc.scalar.copy(out=h_sb[:, 0:BANK], in_=h_bank[0][:])
+            nc.vector.tensor_copy(out=h_sb[:, BANK:N], in_=h_bank[1][:])
+            a = stage.tile([P, N], F32)
+            for c in range(HALVES):
+                cols = slice(c * BANK, (c + 1) * BANK)
+                nc.vector.tensor_tensor(out=a[:, cols], in0=ht_bank[c][:], in1=h_sb[:, cols], op=MULT)
+            sq = stage.tile([P, N], F32)
+            row_sum = stage.tile([P, 1], F32)
+            nc.scalar.activation(out=sq[:], in_=a[:], func=SQUARE, accum_out=row_sum[:])
+            inv_sum = stage.tile([P, 1], F32)
+            nc.vector.reciprocal(out=inv_sum[:], in_=row_sum[:])
+            adj = stage.tile([P, N], F32)
+            nc.gpsimd.tensor_scalar(
+                out=adj[:], in0=sq[:], scalar1=inv_sum[:, 0:1], scalar2=0.0, op0=MULT, op1=ADD
+            )
+            nc.sync.dma_start(out=out[rows, :], in_=adj[:])

@@ -22,6 +22,7 @@ PASSES = D // K_PASS
 ROW_TILES = N // P
 BANK = 512
 HALVES = N // BANK
+TILES_PER_HALF = BANK // P
 
 FLOPS = 2 * N * N * D
 
@@ -30,9 +31,10 @@ def tile_gcn_pa_kernel(tc, x, W1_words, W1_scales, out):
     nc = tc.nc
     with ExitStack() as ctx:
         keep = ctx.enter_context(tc.tile_pool(name="keep", bufs=1))
-        x_pool = ctx.enter_context(tc.tile_pool(name="x_pool", bufs=ROW_TILES))
+        per_tile = ctx.enter_context(tc.tile_pool(name="per_tile", bufs=ROW_TILES))
         stage = ctx.enter_context(tc.tile_pool(name="stage", bufs=3))
         psum = ctx.enter_context(tc.psum_pool(name="psum", bufs=8))
+        ctx.enter_context(tc.manual_schedule())
 
         identity = keep.tile([P, P], F32)
         make_identity(nc, identity[:])
@@ -45,7 +47,7 @@ def tile_gcn_pa_kernel(tc, x, W1_words, W1_scales, out):
 
         x_rows = []
         for i in range(ROW_TILES):
-            x_tile = x_pool.tile([P, D], BF16, tag="x_tile")
+            x_tile = per_tile.tile([P, D], BF16, tag="x_tile")
             nc.sync.dma_start(out=x_tile[:], in_=x[i * P : (i + 1) * P, :])
             x_rows.append(x_tile)
         for quad in range(4):
@@ -53,10 +55,11 @@ def tile_gcn_pa_kernel(tc, x, W1_words, W1_scales, out):
                 out=w_scales[32 * quad : 32 * quad + 4, :, :].bitcast(I32),
                 in_=W1_scales[:, 4 * quad : 4 * quad + 4, :].rearrange("g r n -> r g n").bitcast(I32),
             )
-        for g in range(PASSES):
+        for c in range(HALVES):
+            cols = slice(c * BANK, (c + 1) * BANK)
             nc.sync.dma_start(
-                out=w_codes[:, g, :].bitcast(I32),
-                in_=W1_words[g].rearrange("p n t -> p (n t)").bitcast(I32),
+                out=w_codes[:, :, cols].bitcast(I32),
+                in_=W1_words[:, :, cols, :].rearrange("g p n t -> p g (n t)").bitcast(I32),
             )
 
         for i in range(ROW_TILES):
@@ -83,53 +86,99 @@ def tile_gcn_pa_kernel(tc, x, W1_words, W1_scales, out):
                     in_=grouped[:, g, :, :].rearrange("p r t -> p (r t)"),
                 )
 
-        for i in range(ROW_TILES):
-            rows = slice(i * P, (i + 1) * P)
-            h_bank = []
-            ht_bank = []
-            for c in range(HALVES):
-                cols = slice(c * BANK, (c + 1) * BANK)
-                h_ps = psum.tile([P, BANK], F32, tag="bank")
-                for g in range(PASSES):
-                    nc.tensor.matmul_mx(
-                        out=h_ps[:],
-                        lhsT=x_codes[:, g, rows].bitcast(FP8X4),
-                        lhsT_scale=x_scales[:, g, rows],
-                        rhs=w_codes[:, g, cols].bitcast(FP8X4),
-                        rhs_scale=w_scales[:, g, cols],
-                        start=(g == 0),
-                        stop=(g == PASSES - 1),
-                    )
-                h_bank.append(h_ps)
-            for c in range(HALVES):
-                cols = slice(c * BANK, (c + 1) * BANK)
-                ht_ps = psum.tile([P, BANK], F32, tag="bank")
-                for g in range(PASSES):
-                    nc.tensor.matmul_mx(
-                        out=ht_ps[:],
-                        lhsT=w_codes[:, g, rows].bitcast(FP8X4),
-                        lhsT_scale=w_scales[:, g, rows],
-                        rhs=x_codes[:, g, cols].bitcast(FP8X4),
-                        rhs_scale=x_scales[:, g, cols],
-                        start=(g == 0),
-                        stop=(g == PASSES - 1),
-                    )
-                ht_bank.append(ht_ps)
+        def product(stat_codes, stat_scales, stat_cols, move_codes, move_scales, move_cols):
+            bank = psum.tile([P, BANK], F32, tag="bank")
+            for g in range(PASSES):
+                nc.tensor.matmul_mx(
+                    out=bank[:],
+                    lhsT=stat_codes[:, g, stat_cols].bitcast(FP8X4),
+                    lhsT_scale=stat_scales[:, g, stat_cols],
+                    rhs=move_codes[:, g, move_cols].bitcast(FP8X4),
+                    rhs_scale=move_scales[:, g, move_cols],
+                    start=(g == 0),
+                    stop=(g == PASSES - 1),
+                )
+            return bank
 
-            h_sb = stage.tile([P, N], F32)
-            nc.scalar.copy(out=h_sb[:, 0:BANK], in_=h_bank[0][:])
-            nc.vector.tensor_copy(out=h_sb[:, BANK:N], in_=h_bank[1][:])
-            a = stage.tile([P, N], F32)
-            for c in range(HALVES):
-                cols = slice(c * BANK, (c + 1) * BANK)
-                nc.vector.tensor_tensor(out=a[:, cols], in0=ht_bank[c][:], in1=h_sb[:, cols], op=MULT)
-            sq = stage.tile([P, N], F32)
+        def tile_rows(i):
+            return slice(i * P, (i + 1) * P)
+
+        def half_cols(c):
+            return slice(c * BANK, (c + 1) * BANK)
+
+        def direct_halves(i):
+            return [c for c in reversed(range(HALVES)) if c >= i // TILES_PER_HALF]
+
+        ht_bank = {}
+        h_bank = {}
+        at_bank = {}
+        ht_sb = {}
+        a = {}
+        sq = {}
+        half_sums = {}
+
+        def products(i):
+            for c in direct_halves(i):
+                ht_bank[i, c] = product(w_codes, w_scales, tile_rows(i), x_codes, x_scales, half_cols(c))
+            for c in direct_halves(i):
+                h_bank[i, c] = product(x_codes, x_scales, tile_rows(i), w_codes, w_scales, half_cols(c))
+            ht_sb[i] = stage.tile([P, N], F32, name="ht_sb")
+            a[i] = per_tile.tile([P, N], F32, name="a")
+            sq[i] = per_tile.tile([P, N], F32, name="sq")
+            half_sums[i] = per_tile.tile([P, HALVES], F32, name="half_sums")
+
+        def transposes():
+            for i in range(TILES_PER_HALF, ROW_TILES):
+                at_bank[i] = psum.tile([P, BANK], F32, name="at", tag="bank")
+                for j in range(TILES_PER_HALF):
+                    nc.tensor.transpose(at_bank[i][:, tile_rows(j)], a[j][:, tile_rows(i)], identity[:])
+
+        def square(i, c, source):
+            nc.scalar.activation(
+                out=sq[i][:, half_cols(c)], in_=source, func=SQUARE, accum_out=half_sums[i][:, c : c + 1]
+            )
+
+        def leave_psum(i, c):
+            if c == 0:
+                nc.scalar.copy(out=ht_sb[i][:, half_cols(c)], in_=ht_bank[i, c][:])
+            else:
+                nc.vector.tensor_copy(out=ht_sb[i][:, half_cols(c)], in_=ht_bank[i, c][:])
+
+        def multiply(i, c):
+            nc.vector.tensor_tensor(
+                out=a[i][:, half_cols(c)], in0=h_bank[i, c][:], in1=ht_sb[i][:, half_cols(c)], op=MULT
+            )
+
+        def normalise(i):
             row_sum = stage.tile([P, 1], F32)
-            nc.scalar.activation(out=sq[:], in_=a[:], func=SQUARE, accum_out=row_sum[:])
+            nc.vector.tensor_tensor(
+                out=row_sum[:], in0=half_sums[i][:, 0:1], in1=half_sums[i][:, 1:2], op=ADD
+            )
             inv_sum = stage.tile([P, 1], F32)
             nc.vector.reciprocal(out=inv_sum[:], in_=row_sum[:])
             adj = stage.tile([P, N], F32)
             nc.gpsimd.tensor_scalar(
-                out=adj[:], in0=sq[:], scalar1=inv_sum[:, 0:1], scalar2=0.0, op0=MULT, op1=ADD
+                out=adj[:], in0=sq[i][:], scalar1=inv_sum[:, 0:1], scalar2=0.0, op0=MULT, op1=ADD
             )
-            nc.sync.dma_start(out=out[rows, :], in_=adj[:])
+            nc.sync.dma_start(out=out[tile_rows(i), :], in_=adj[:])
+
+        for new in range(ROW_TILES + 1):
+            old = new - 1
+            if new < ROW_TILES:
+                products(new)
+            if new == TILES_PER_HALF:
+                transposes()
+            if old >= 0:
+                for c in direct_halves(old):
+                    square(old, c, a[old][:, half_cols(c)])
+            if new < ROW_TILES:
+                if new >= TILES_PER_HALF:
+                    square(new, 0, at_bank[new][:])
+                for c in direct_halves(new):
+                    leave_psum(new, c)
+                multiply(new, direct_halves(new)[0])
+            if old >= 0:
+                normalise(old)
+            if new < ROW_TILES:
+                for c in direct_halves(new)[1:]:
+                    multiply(new, c)

@@ -10,6 +10,7 @@ U32 = mybir.dt.uint32
 U8 = mybir.dt.uint8
 FP8X4 = mybir.dt.float8_e4m3fn_x4
 SQUARE = mybir.ActivationFunctionType.Square
+IDENTITY = mybir.ActivationFunctionType.Identity
 MULT = mybir.AluOpType.mult
 ADD = mybir.AluOpType.add
 
@@ -23,6 +24,10 @@ ROW_TILES = N // P
 BANK = 512
 HALVES = N // BANK
 TILES_PER_HALF = BANK // P
+
+LEFT, RIGHT = 0, 1
+LAG = 2
+TRANSPOSE_AFTER = (TILES_PER_HALF + LAG, RIGHT)
 
 FLOPS = 2 * N * N * D
 
@@ -45,25 +50,29 @@ def tile_gcn_pa_kernel(tc, x, W1_words, W1_scales, out):
         w_scales = keep.tile([P, PASSES, N], U8, align_bytes=64)
         nc.vector.memset(w_scales[:].bitcast(I32), 0)
 
+        def tile_rows(i):
+            return slice(i * P, (i + 1) * P)
+
+        def half_cols(c):
+            return slice(c * BANK, (c + 1) * BANK)
+
         x_rows = []
         for i in range(ROW_TILES):
             x_tile = per_tile.tile([P, D], BF16, tag="x_tile")
-            nc.sync.dma_start(out=x_tile[:], in_=x[i * P : (i + 1) * P, :])
+            nc.sync.dma_start(out=x_tile[:], in_=x[tile_rows(i), :])
             x_rows.append(x_tile)
         for quad in range(4):
             nc.sync.dma_start(
                 out=w_scales[32 * quad : 32 * quad + 4, :, :].bitcast(I32),
                 in_=W1_scales[:, 4 * quad : 4 * quad + 4, :].rearrange("g r n -> r g n").bitcast(I32),
             )
-        for c in range(HALVES):
-            cols = slice(c * BANK, (c + 1) * BANK)
+        for c in (LEFT, RIGHT):
             nc.sync.dma_start(
-                out=w_codes[:, :, cols].bitcast(I32),
-                in_=W1_words[:, :, cols, :].rearrange("g p n t -> p g (n t)").bitcast(I32),
+                out=w_codes[:, :, half_cols(c)].bitcast(I32),
+                in_=W1_words[:, :, half_cols(c), :].rearrange("g p n t -> p g (n t)").bitcast(I32),
             )
 
         for i in range(ROW_TILES):
-            rows = slice(i * P, (i + 1) * P)
             x_words = x_rows[i][:].bitcast(F32)
             xt = psum.tile([P, BANK], F32, tag="bank")
             for g in range(PASSES):
@@ -81,8 +90,8 @@ def tile_gcn_pa_kernel(tc, x, W1_words, W1_scales, out):
             )
             for g in range(PASSES):
                 nc.vector.quantize_mx(
-                    out=x_codes[:, g, rows].bitcast(FP8X4),
-                    scales=x_scales[:, g, rows],
+                    out=x_codes[:, g, tile_rows(i)].bitcast(FP8X4),
+                    scales=x_scales[:, g, tile_rows(i)],
                     in_=grouped[:, g, :, :].rearrange("p r t -> p (r t)"),
                 )
 
@@ -100,14 +109,12 @@ def tile_gcn_pa_kernel(tc, x, W1_words, W1_scales, out):
                 )
             return bank
 
-        def tile_rows(i):
-            return slice(i * P, (i + 1) * P)
-
-        def half_cols(c):
-            return slice(c * BANK, (c + 1) * BANK)
-
-        def direct_halves(i):
-            return [c for c in reversed(range(HALVES)) if c >= i // TILES_PER_HALF]
+        halves = []
+        for i in range(ROW_TILES + 1):
+            if i < TILES_PER_HALF:
+                halves.append((i, LEFT))
+            if i >= 1:
+                halves.append((i - 1, RIGHT))
 
         ht_bank = {}
         h_bank = {}
@@ -116,16 +123,17 @@ def tile_gcn_pa_kernel(tc, x, W1_words, W1_scales, out):
         a = {}
         sq = {}
         half_sums = {}
-
-        def products(i):
-            for c in direct_halves(i):
-                ht_bank[i, c] = product(w_codes, w_scales, tile_rows(i), x_codes, x_scales, half_cols(c))
-            for c in direct_halves(i):
-                h_bank[i, c] = product(x_codes, x_scales, tile_rows(i), w_codes, w_scales, half_cols(c))
-            ht_sb[i] = stage.tile([P, N], F32, name="ht_sb")
+        for i in range(ROW_TILES):
             a[i] = per_tile.tile([P, N], F32, name="a")
             sq[i] = per_tile.tile([P, N], F32, name="sq")
             half_sums[i] = per_tile.tile([P, HALVES], F32, name="half_sums")
+
+        def lower(i):
+            return i >= TILES_PER_HALF
+
+        def products(i, c):
+            ht_bank[i, c] = product(w_codes, w_scales, tile_rows(i), x_codes, x_scales, half_cols(c))
+            h_bank[i, c] = product(x_codes, x_scales, tile_rows(i), w_codes, w_scales, half_cols(c))
 
         def transposes():
             for i in range(TILES_PER_HALF, ROW_TILES):
@@ -133,52 +141,49 @@ def tile_gcn_pa_kernel(tc, x, W1_words, W1_scales, out):
                 for j in range(TILES_PER_HALF):
                     nc.tensor.transpose(at_bank[i][:, tile_rows(j)], a[j][:, tile_rows(i)], identity[:])
 
+        def leave_psum(i, c):
+            ht_sb[i, c] = stage.tile([P, BANK], F32, name="ht_sb")
+            if c == LEFT:
+                nc.scalar.copy(out=ht_sb[i, c][:], in_=ht_bank[i, c][:])
+            else:
+                nc.vector.tensor_copy(out=ht_sb[i, c][:], in_=ht_bank[i, c][:])
+
+        def multiply(i, c):
+            nc.vector.tensor_tensor(out=a[i][:, half_cols(c)], in0=h_bank[i, c][:], in1=ht_sb[i, c][:], op=MULT)
+
         def square(i, c, source):
             nc.scalar.activation(
                 out=sq[i][:, half_cols(c)], in_=source, func=SQUARE, accum_out=half_sums[i][:, c : c + 1]
             )
 
-        def leave_psum(i, c):
-            if c == 0:
-                nc.scalar.copy(out=ht_sb[i][:, half_cols(c)], in_=ht_bank[i, c][:])
-            else:
-                nc.vector.tensor_copy(out=ht_sb[i][:, half_cols(c)], in_=ht_bank[i, c][:])
-
-        def multiply(i, c):
-            nc.vector.tensor_tensor(
-                out=a[i][:, half_cols(c)], in0=h_bank[i, c][:], in1=ht_sb[i][:, half_cols(c)], op=MULT
-            )
-
         def normalise(i):
             row_sum = stage.tile([P, 1], F32)
-            nc.vector.tensor_tensor(
-                out=row_sum[:], in0=half_sums[i][:, 0:1], in1=half_sums[i][:, 1:2], op=ADD
+            nc.scalar.activation(
+                out=row_sum[:], in_=half_sums[i][:, LEFT : LEFT + 1], func=IDENTITY, bias=half_sums[i][:, RIGHT : RIGHT + 1]
             )
             inv_sum = stage.tile([P, 1], F32)
             nc.vector.reciprocal(out=inv_sum[:], in_=row_sum[:])
-            adj = stage.tile([P, N], F32)
-            nc.gpsimd.tensor_scalar(
-                out=adj[:], in0=sq[i][:], scalar1=inv_sum[:, 0:1], scalar2=0.0, op0=MULT, op1=ADD
-            )
-            nc.sync.dma_start(out=out[tile_rows(i), :], in_=adj[:])
+            if lower(i):
+                nc.vector.tensor_scalar(out=sq[i][:], in0=sq[i][:], scalar1=inv_sum[:, 0:1], scalar2=None, op0=MULT)
+            else:
+                nc.gpsimd.tensor_scalar(
+                    out=sq[i][:], in0=sq[i][:], scalar1=inv_sum[:, 0:1], scalar2=0.0, op0=MULT, op1=ADD
+                )
+            nc.sync.dma_start(out=out[tile_rows(i), :], in_=sq[i][:])
 
-        for new in range(ROW_TILES + 1):
-            old = new - 1
-            if new < ROW_TILES:
-                products(new)
-            if new == TILES_PER_HALF:
-                transposes()
-            if old >= 0:
-                for c in direct_halves(old):
-                    square(old, c, a[old][:, half_cols(c)])
-            if new < ROW_TILES:
-                if new >= TILES_PER_HALF:
-                    square(new, 0, at_bank[new][:])
-                for c in direct_halves(new):
-                    leave_psum(new, c)
-                multiply(new, direct_halves(new)[0])
-            if old >= 0:
-                normalise(old)
-            if new < ROW_TILES:
-                for c in direct_halves(new)[1:]:
-                    multiply(new, c)
+        for step in range(len(halves) + LAG):
+            if step < len(halves):
+                i, c = halves[step]
+                products(i, c)
+                if (i, c) == TRANSPOSE_AFTER:
+                    transposes()
+                leave_psum(i, c)
+            if step >= LAG:
+                i_old, c_old = halves[step - LAG]
+                if lower(i_old):
+                    square(i_old, LEFT, at_bank[i_old][:])
+                square(i_old, c_old, a[i_old][:, half_cols(c_old)])
+            if step < len(halves):
+                multiply(i, c)
+            if step >= LAG and c_old == RIGHT:
+                normalise(i_old)

@@ -10,9 +10,9 @@ U32 = mybir.dt.uint32
 U8 = mybir.dt.uint8
 FP8X4 = mybir.dt.float8_e4m3fn_x4
 SQUARE = mybir.ActivationFunctionType.Square
-IDENTITY = mybir.ActivationFunctionType.Identity
 MULT = mybir.AluOpType.mult
 ADD = mybir.AluOpType.add
+AXIS_X = mybir.AxisListType.X
 
 P = 128
 PACK = 4
@@ -20,61 +20,88 @@ K_PASS = P * PACK
 N = 1024
 D = 1024
 PASSES = D // K_PASS
-ROW_TILES = N // P
+TILES = N // P
 BANK = 512
-HALVES = N // BANK
-TILES_PER_HALF = BANK // P
-
-LEFT, RIGHT = 0, 1
-LAG = 2
-TRANSPOSE_AFTER = (TILES_PER_HALF + LAG, RIGHT)
+BANKS = 8
+HALF = BANK // P
 
 FLOPS = 2 * N * N * D
+SCALED_BY_GPSIMD = 5
 
 
 def tile_gcn_pa_kernel(tc, x, W1_words, W1_scales, out):
     nc = tc.nc
     with ExitStack() as ctx:
         keep = ctx.enter_context(tc.tile_pool(name="keep", bufs=1))
-        per_tile = ctx.enter_context(tc.tile_pool(name="per_tile", bufs=ROW_TILES))
-        stage = ctx.enter_context(tc.tile_pool(name="stage", bufs=3))
-        psum = ctx.enter_context(tc.psum_pool(name="psum", bufs=8))
+        psum = ctx.enter_context(tc.psum_pool(name="psum", bufs=1))
         ctx.enter_context(tc.manual_schedule())
 
-        identity = keep.tile([P, P], F32)
+        identity = keep.tile([P, P], F32, name="identity")
         make_identity(nc, identity[:])
 
-        x_codes = keep.tile([P, PASSES, N], U32, align_bytes=64)
-        x_scales = keep.tile([P, PASSES, N], U8, align_bytes=64)
-        w_codes = keep.tile([P, PASSES, N], U32, align_bytes=64)
-        w_scales = keep.tile([P, PASSES, N], U8, align_bytes=64)
-        nc.vector.memset(w_scales[:].bitcast(I32), 0)
+        x_codes = keep.tile([P, PASSES, N], U32, name="x_codes", align_bytes=64)
+        x_scales = keep.tile([P, PASSES, N], U8, name="x_scales", align_bytes=64)
+        w_codes = keep.tile([P, PASSES, N], U32, name="w_codes", align_bytes=64)
+        w_scales = keep.tile([P, PASSES, N], U8, name="w_scales", align_bytes=64)
 
-        def tile_rows(i):
-            return slice(i * P, (i + 1) * P)
+        x_rows = [keep.tile([P, D], BF16, name="x_rows%d" % i) for i in range(TILES)]
+        grouped = [keep.tile([P, PASSES, P, PACK], BF16, name="grouped%d" % i, align_bytes=64) for i in range(TILES)]
+        a = [keep.tile([P, N], F32, name="a%d" % i) for i in range(TILES)]
+        sq = [keep.tile([P, N], F32, name="sq%d" % i) for i in range(TILES)]
+        sums = [keep.tile([P, 4], F32, name="sums%d" % i) for i in range(TILES)]
+        total = [keep.tile([P, 1], F32, name="total%d" % i) for i in range(TILES)]
+        inv = [keep.tile([P, 1], F32, name="inv%d" % i) for i in range(TILES)]
 
-        def half_cols(c):
-            return slice(c * BANK, (c + 1) * BANK)
+        def blocks(c0, c1):
+            return slice(c0 * P, c1 * P)
 
-        x_rows = []
-        for i in range(ROW_TILES):
-            x_tile = per_tile.tile([P, D], BF16, tag="x_tile")
-            nc.sync.dma_start(out=x_tile[:], in_=x[tile_rows(i), :])
-            x_rows.append(x_tile)
-        for quad in range(4):
+        steps = {}
+        order = {"PE": [], "V": [], "S": [], "G": [], "SP": []}
+        bank_of = {}
+        bank_state = {"count": 0}
+        bank_readers = {}
+
+        def step(engine, name, needs, fn):
+            steps[name] = (list(needs), fn)
+            order[engine].append(name)
+
+        def claim_bank(key, readers):
+            k = bank_state["count"] % BANKS
+            bank_state["count"] += 1
+            former = bank_readers.get(k, [])
+            bank_readers[k] = list(readers)
+            return k, former
+
+        def new_bank(key, k):
+            bank_of[key] = psum.tile([P, BANK], F32, name="ps_" + key, tag="bank%d" % k)
+            return bank_of[key]
+
+        def load_x(i):
+            nc.sync.dma_start(out=x_rows[i][:], in_=x[blocks(i, i + 1), :])
+
+        def load_w_scales(quad):
             nc.sync.dma_start(
                 out=w_scales[32 * quad : 32 * quad + 4, :, :].bitcast(I32),
                 in_=W1_scales[:, 4 * quad : 4 * quad + 4, :].rearrange("g r n -> r g n").bitcast(I32),
             )
-        for c in (LEFT, RIGHT):
+
+        def load_w(c):
             nc.sync.dma_start(
-                out=w_codes[:, :, half_cols(c)].bitcast(I32),
-                in_=W1_words[:, :, half_cols(c), :].rearrange("g p n t -> p g (n t)").bitcast(I32),
+                out=w_codes[:, :, blocks(HALF * c, HALF * (c + 1))].bitcast(I32),
+                in_=W1_words[:, :, blocks(HALF * c, HALF * (c + 1)), :].rearrange("g p n t -> p g (n t)").bitcast(I32),
             )
 
-        for i in range(ROW_TILES):
+        step("V", "zero", [], lambda: nc.vector.memset(w_scales[:].bitcast(I32), 0))
+        for i in range(TILES):
+            step("SP", "ldx%d" % i, [], lambda i=i: load_x(i))
+        for quad in range(4):
+            step("SP", "lds%d" % quad, ["zero"], lambda quad=quad: load_w_scales(quad))
+        for c in range(2):
+            step("SP", "ldw%d" % c, [], lambda c=c: load_w(c))
+
+        def transpose_x(i, k):
             x_words = x_rows[i][:].bitcast(F32)
-            xt = psum.tile([P, BANK], F32, tag="bank")
+            xt = new_bank("tx%d" % i, k)
             for g in range(PASSES):
                 for u in range(2):
                     plane = 2 * g + u
@@ -83,107 +110,172 @@ def tile_gcn_pa_kernel(tc, x, W1_words, W1_scales, out):
                         x_words[:, 256 * g + u : 256 * (g + 1) : 2],
                         identity[:],
                     )
-            grouped = stage.tile([P, PASSES, P, PACK], BF16, align_bytes=64)
+
+        def group_x(i):
             nc.scalar.copy(
-                out=grouped[:].bitcast(F32),
-                in_=xt[:].rearrange("p (g u r) -> p g r u", g=PASSES, u=2),
+                out=grouped[i][:].bitcast(F32),
+                in_=bank_of["tx%d" % i][:].rearrange("p (g u r) -> p g r u", g=PASSES, u=2),
             )
+
+        def quantise_x(i):
             for g in range(PASSES):
                 nc.vector.quantize_mx(
-                    out=x_codes[:, g, tile_rows(i)].bitcast(FP8X4),
-                    scales=x_scales[:, g, tile_rows(i)],
-                    in_=grouped[:, g, :, :].rearrange("p r t -> p (r t)"),
+                    out=x_codes[:, g, blocks(i, i + 1)].bitcast(FP8X4),
+                    scales=x_scales[:, g, blocks(i, i + 1)],
+                    in_=grouped[i][:, g, :, :].rearrange("p r t -> p (r t)"),
                 )
 
-        def product(stat_codes, stat_scales, stat_cols, move_codes, move_scales, move_cols):
-            bank = psum.tile([P, BANK], F32, tag="bank")
-            for g in range(PASSES):
-                nc.tensor.matmul_mx(
-                    out=bank[:],
-                    lhsT=stat_codes[:, g, stat_cols].bitcast(FP8X4),
-                    lhsT_scale=stat_scales[:, g, stat_cols],
-                    rhs=move_codes[:, g, move_cols].bitcast(FP8X4),
-                    rhs_scale=move_scales[:, g, move_cols],
-                    start=(g == 0),
-                    stop=(g == PASSES - 1),
-                )
-            return bank
+        for i in range(TILES):
+            k, former = claim_bank("tx%d" % i, ["ex%d" % i])
+            step("PE", "tx%d" % i, ["ldx%d" % i] + former, lambda i=i, k=k: transpose_x(i, k))
+            step("S", "ex%d" % i, ["tx%d" % i], lambda i=i: group_x(i))
+            step("V", "qx%d" % i, ["ex%d" % i], lambda i=i: quantise_x(i))
 
-        halves = []
-        for i in range(ROW_TILES + 1):
-            if i < TILES_PER_HALF:
-                halves.append((i, LEFT))
-            if i >= 1:
-                halves.append((i - 1, RIGHT))
+        def product(bank, stat_codes, stat_scales, stat_block, move_codes, move_scales, c0, c1):
+            widths = {1: [1], 2: [2], 3: [2, 1], 4: [4]}[c1 - c0]
+            start = 0
+            for width in widths:
+                for g in range(PASSES):
+                    nc.tensor.matmul_mx(
+                        out=bank[:, blocks(start, start + width)],
+                        lhsT=stat_codes[:, g, blocks(stat_block, stat_block + 1)].bitcast(FP8X4),
+                        lhsT_scale=stat_scales[:, g, blocks(stat_block, stat_block + 1)],
+                        rhs=move_codes[:, g, blocks(c0 + start, c0 + start + width)].bitcast(FP8X4),
+                        rhs_scale=move_scales[:, g, blocks(c0 + start, c0 + start + width)],
+                        start=(g == 0),
+                        stop=(g == PASSES - 1),
+                    )
+                start += width
 
-        ht_bank = {}
-        h_bank = {}
-        at_bank = {}
         ht_sb = {}
-        a = {}
-        sq = {}
-        half_sums = {}
-        for i in range(ROW_TILES):
-            a[i] = per_tile.tile([P, N], F32, name="a")
-            sq[i] = per_tile.tile([P, N], F32, name="sq")
-            half_sums[i] = per_tile.tile([P, HALVES], F32, name="half_sums")
 
-        def lower(i):
-            return i >= TILES_PER_HALF
+        def products(u, i, c0, c1, k_ht, k_h):
+            product(new_bank("ht" + u, k_ht), w_codes, w_scales, i, x_codes, x_scales, c0, c1)
+            product(new_bank("h" + u, k_h), x_codes, x_scales, i, w_codes, w_scales, c0, c1)
 
-        def products(i, c):
-            ht_bank[i, c] = product(w_codes, w_scales, tile_rows(i), x_codes, x_scales, half_cols(c))
-            h_bank[i, c] = product(x_codes, x_scales, tile_rows(i), w_codes, w_scales, half_cols(c))
-
-        def transposes():
-            for i in range(TILES_PER_HALF, ROW_TILES):
-                at_bank[i] = psum.tile([P, BANK], F32, name="at", tag="bank")
-                for j in range(TILES_PER_HALF):
-                    nc.tensor.transpose(at_bank[i][:, tile_rows(j)], a[j][:, tile_rows(i)], identity[:])
-
-        def leave_psum(i, c):
-            ht_sb[i, c] = stage.tile([P, BANK], F32, name="ht_sb")
-            if c == LEFT:
-                nc.scalar.copy(out=ht_sb[i, c][:], in_=ht_bank[i, c][:])
+        def leave_psum(u, engine, width):
+            if engine == "S":
+                nc.scalar.copy(out=ht_sb[u][:, : width * P], in_=bank_of["ht" + u][:, : width * P])
             else:
-                nc.vector.tensor_copy(out=ht_sb[i, c][:], in_=ht_bank[i, c][:])
+                nc.vector.tensor_copy(out=ht_sb[u][:, : width * P], in_=bank_of["ht" + u][:, : width * P])
 
-        def multiply(i, c):
-            nc.vector.tensor_tensor(out=a[i][:, half_cols(c)], in0=h_bank[i, c][:], in1=ht_sb[i, c][:], op=MULT)
-
-        def square(i, c, source):
-            nc.scalar.activation(
-                out=sq[i][:, half_cols(c)], in_=source, func=SQUARE, accum_out=half_sums[i][:, c : c + 1]
+        def multiply(u, i, c0, c1):
+            nc.vector.tensor_tensor(
+                out=a[i][:, blocks(c0, c1)], in0=bank_of["h" + u][:, : (c1 - c0) * P], in1=ht_sb[u][:, : (c1 - c0) * P], op=MULT
             )
 
-        def normalise(i):
-            row_sum = stage.tile([P, 1], F32)
-            nc.scalar.activation(
-                out=row_sum[:], in_=half_sums[i][:, LEFT : LEFT + 1], func=IDENTITY, bias=half_sums[i][:, RIGHT : RIGHT + 1]
-            )
-            inv_sum = stage.tile([P, 1], F32)
-            nc.vector.reciprocal(out=inv_sum[:], in_=row_sum[:])
-            if lower(i):
-                nc.vector.tensor_scalar(out=sq[i][:], in0=sq[i][:], scalar1=inv_sum[:, 0:1], scalar2=None, op0=MULT)
-            else:
-                nc.gpsimd.tensor_scalar(
-                    out=sq[i][:], in0=sq[i][:], scalar1=inv_sum[:, 0:1], scalar2=0.0, op0=MULT, op1=ADD
-                )
-            nc.sync.dma_start(out=out[tile_rows(i), :], in_=sq[i][:])
+        def square(i, c0, c1, source, slot):
+            nc.scalar.activation(out=sq[i][:, blocks(c0, c1)], in_=source, func=SQUARE, accum_out=sums[i][:, slot : slot + 1])
 
-        for step in range(len(halves) + LAG):
-            if step < len(halves):
-                i, c = halves[step]
-                products(i, c)
-                if (i, c) == TRANSPOSE_AFTER:
-                    transposes()
-                leave_psum(i, c)
-            if step >= LAG:
-                i_old, c_old = halves[step - LAG]
-                if lower(i_old):
-                    square(i_old, LEFT, at_bank[i_old][:])
-                square(i_old, c_old, a[i_old][:, half_cols(c_old)])
-            if step < len(halves):
-                multiply(i, c)
-            if step >= LAG and c_old == RIGHT:
-                normalise(i_old)
+        def transposes(key, j, i0, i1, k):
+            at = new_bank(key, k)
+            for i in range(i0, i1):
+                nc.tensor.transpose(at[:, blocks(i - i0, i - i0 + 1)], a[i][:, blocks(j, j + 1)], identity[:])
+
+        def reciprocal(i, slots):
+            nc.vector.tensor_reduce(out=total[i][:], in_=sums[i][:, :slots], axis=AXIS_X, op=ADD)
+            nc.vector.reciprocal(out=inv[i][:], in_=total[i][:])
+
+        def scale(i, engine):
+            if engine == "V":
+                nc.vector.tensor_scalar(out=sq[i][:], in0=sq[i][:], scalar1=inv[i][:, 0:1], scalar2=None, op0=MULT)
+            else:
+                nc.gpsimd.tensor_scalar(out=sq[i][:], in0=sq[i][:], scalar1=inv[i][:, 0:1], scalar2=0.0, op0=MULT, op1=ADD)
+
+        def store(i):
+            nc.sync.dma_start(out=out[blocks(i, i + 1), :], in_=sq[i][:])
+
+        def left(i):
+            return "%d_%d" % (i, i)
+
+        def right(i):
+            return "%d_%d" % (i, max(i, HALF))
+
+        def unit_of(i, j):
+            return left(i) if j < HALF else right(i)
+
+        row_parts = [[] for i in range(TILES)]
+
+        def plan_products(i, c0, c1):
+            u = "%d_%d" % (i, c0)
+            ht_sb[u] = keep.tile([P, BANK], F32, name="ht_sb%d_%d" % (i, c0))
+            k_ht, former_ht = claim_bank("ht" + u, ["e" + u])
+            k_h, former_h = claim_bank("h" + u, ["m" + u])
+            needs = ["lds3", "ldw%d" % (i // HALF), "ldw%d" % (c0 // HALF), "qx%d" % i] + ["qx%d" % j for j in range(c0, c1)]
+            step("PE", "p" + u, needs + former_ht + former_h, lambda: products(u, i, c0, c1, k_ht, k_h))
+
+        def plan_transposes(j, i0, i1):
+            key = "t%d_%d" % (j, i0)
+            k, former = claim_bank(key, ["x%d_%d" % (j, i0)])
+            step("PE", key, ["m" + unit_of(i, j) for i in range(i0, i1)] + former, lambda: transposes(key, j, i0, i1, k))
+
+        def plan_leave(i, c0, c1, engine):
+            u = "%d_%d" % (i, c0)
+            step(engine, "e" + u, ["p" + u], lambda: leave_psum(u, engine, c1 - c0))
+
+        def plan_multiply(i, c0, c1):
+            u = "%d_%d" % (i, c0)
+            step("V", "m" + u, ["e" + u, "p" + u], lambda: multiply(u, i, c0, c1))
+
+        def plan_square(i, c0, c1):
+            u = "%d_%d" % (i, c0)
+            slot = len(row_parts[i])
+            row_parts[i].append("q" + u)
+            step("S", "q" + u, ["m" + u], lambda: square(i, c0, c1, a[i][:, blocks(c0, c1)], slot))
+
+        def plan_square_transposed(j, i0, i1):
+            key = "%d_%d" % (j, i0)
+            slot = len(row_parts[j])
+            row_parts[j].append("x" + key)
+            step("S", "x" + key, ["t" + key], lambda: square(j, i0, i1, bank_of["t" + key][:, : (i1 - i0) * P], slot))
+
+        def plan_normalise(i):
+            engine = "G" if i < SCALED_BY_GPSIMD else "V"
+            slots = len(row_parts[i])
+            step("V", "r%d" % i, row_parts[i], lambda: reciprocal(i, slots))
+            step(engine, "n%d" % i, ["r%d" % i], lambda: scale(i, engine))
+            step("SP", "st%d" % i, ["n%d" % i], lambda: store(i))
+
+        for i in range(TILES + 1):
+            if i < HALF:
+                plan_products(i, i, HALF)
+            if i < TILES:
+                plan_products(i, max(i, HALF), TILES)
+                if i >= 1:
+                    plan_transposes(i, 0, min(i, HALF))
+                if i > HALF:
+                    plan_transposes(i, HALF, i)
+            if i < HALF:
+                plan_leave(i, i, HALF, "S")
+            if i >= 1:
+                plan_square(i - 1, max(i - 1, HALF), TILES)
+            if 1 <= i < TILES:
+                plan_square_transposed(i, 0, min(i, HALF))
+            if HALF < i < TILES:
+                plan_square_transposed(i, HALF, i)
+            if i < HALF:
+                plan_square(i, i, HALF)
+            if i < HALF:
+                plan_multiply(i, i, HALF)
+            if i < TILES:
+                plan_leave(i, max(i, HALF), TILES, "V")
+                plan_multiply(i, max(i, HALF), TILES)
+            if i >= 1:
+                plan_normalise(i - 1)
+
+        written = set()
+        position = dict((engine, 0) for engine in order)
+        left_to_write = len(steps)
+        while left_to_write > 0:
+            before = left_to_write
+            for engine in order:
+                while position[engine] < len(order[engine]):
+                    name = order[engine][position[engine]]
+                    needs, fn = steps[name]
+                    if not all(need in written for need in needs):
+                        break
+                    fn()
+                    written.add(name)
+                    position[engine] += 1
+                    left_to_write -= 1
+            assert left_to_write < before, "the engines' orders wait for each other"

@@ -26,7 +26,89 @@ BANKS = 8
 HALF = BANK // P
 
 FLOPS = 2 * N * N * D
-SCALED_BY_GPSIMD = 5
+COPY = mybir.ActivationFunctionType.Copy
+X_LEAVES_BY_VECTOR = ()
+LEAVES_BY_SCALAR = ("0_0", "1_1", "2_2", "3_3")
+ONE_SQUARE_A_ROW = False
+SCALE_PARTS = [[("G" if i < 5 else "V", 0, TILES)] for i in range(TILES)]
+STORE_PARTS = [[(0, TILES, [0])] for i in range(TILES)]
+LOADS = ["ldx%d" % i for i in range(TILES)] + ["lds%d" % q for q in range(4)] + ["ldw0", "ldw1"]
+SQUARES_TRANSPOSED = ()
+H_FIRST = ()
+
+
+def make_order(units_of, unit):
+    order = {"PE": [], "V": ["zero"], "S": [], "G": [], "SP": []}
+    order["SP"] += LOADS
+    for i in range(TILES):
+        order["PE"].append("tx%d" % i)
+        order["V" if i in X_LEAVES_BY_VECTOR else "S"].append("ex%d" % i)
+        order["V"].append("qx%d" % i)
+    def scale_and_store(i):
+        for part, (engine, c0, c1) in enumerate(SCALE_PARTS[i]):
+            order[engine].append("n%d_%d" % (i, part))
+        for part in range(len(STORE_PARTS[i])):
+            order["SP"].append("st%d_%d" % (i, part))
+    def by_vector(i):
+        return 0 <= i < TILES and SCALE_PARTS[i][0][0] == "V"
+    for i in range(TILES + 2):
+        left = unit(i, i)
+        right = unit(i, max(i, HALF))
+        before = unit(i - 1, max(i - 1, HALF))
+        if i < HALF:
+            order["PE"] += ["pt" + left, "ph" + left] + (["ph" + right, "pt" + right] if i in H_FIRST else ["pt" + right, "ph" + right])
+        elif i < TILES:
+            order["PE"] += ["pt" + right, "ph" + right]
+        if 1 <= i < TILES:
+            order["PE"].append("t" + unit(i, 0))
+        if HALF < i < TILES:
+            order["PE"].append("t" + unit(i, HALF))
+        if i < HALF:
+            order["S"].append("e" + left)
+        if i < TILES and right in LEAVES_BY_SCALAR:
+            order["S"].append("e" + right)
+        if 1 <= i <= TILES:
+            order["S"].append("q" + before)
+        if i < HALF:
+            order["S"].append("q" + left)
+        if 1 <= i < TILES:
+            order["S"].append("x" + unit(i, 0))
+        if HALF < i < TILES:
+            order["S"].append("x" + unit(i, HALF))
+        if i < HALF:
+            order["V"].append("m" + left)
+        if i < TILES and right not in LEAVES_BY_SCALAR:
+            order["V"].append("e" + right)
+        if by_vector(i - 2):
+            scale_and_store(i - 2)
+        if 1 <= i <= TILES:
+            order["V"].append("rs%d" % (i - 1))
+        if i < TILES:
+            order["V"].append("m" + right)
+        if 1 <= i <= TILES:
+            order["V"].append("r%d" % (i - 1))
+            if not by_vector(i - 1):
+                scale_and_store(i - 1)
+    return order
+
+
+def write_in_order(steps, order):
+    written = set()
+    position = dict((engine, 0) for engine in order)
+    left_to_write = len(steps)
+    while left_to_write > 0:
+        before = left_to_write
+        for engine in order:
+            while position[engine] < len(order[engine]):
+                name = order[engine][position[engine]]
+                needs, fn = steps[name]
+                if not all(need in written for need in needs):
+                    break
+                fn()
+                written.add(name)
+                position[engine] += 1
+                left_to_write -= 1
+        assert left_to_write < before, "the engines' orders wait for each other"
 
 
 def tile_gcn_pa_kernel(tc, x, W1_words, W1_scales, out):
@@ -51,30 +133,26 @@ def tile_gcn_pa_kernel(tc, x, W1_words, W1_scales, out):
         sums = [keep.tile([P, 4], F32, name="sums%d" % i) for i in range(TILES)]
         total = [keep.tile([P, 1], F32, name="total%d" % i) for i in range(TILES)]
         inv = [keep.tile([P, 1], F32, name="inv%d" % i) for i in range(TILES)]
+        ht_sb = {}
 
         def blocks(c0, c1):
             return slice(c0 * P, c1 * P)
 
         steps = {}
-        order = {"PE": [], "V": [], "S": [], "G": [], "SP": []}
+        engine_of = {}
+        fills = {}
+        bank_number = {}
         bank_of = {}
-        bank_state = {"count": 0}
-        bank_readers = {}
 
-        def step(engine, name, needs, fn):
+        def step(engine, name, needs, fn, readers=None):
             steps[name] = (list(needs), fn)
-            order[engine].append(name)
+            engine_of[name] = engine
+            if readers is not None:
+                fills[name] = readers
 
-        def claim_bank(key, readers):
-            k = bank_state["count"] % BANKS
-            bank_state["count"] += 1
-            former = bank_readers.get(k, [])
-            bank_readers[k] = list(readers)
-            return k, former
-
-        def new_bank(key, k):
-            bank_of[key] = psum.tile([P, BANK], F32, name="ps_" + key, tag="bank%d" % k)
-            return bank_of[key]
+        def new_bank(name):
+            bank_of[name] = psum.tile([P, BANK], F32, name="ps_" + name, tag="bank%d" % bank_number[name])
+            return bank_of[name]
 
         def load_x(i):
             nc.sync.dma_start(out=x_rows[i][:], in_=x[blocks(i, i + 1), :])
@@ -99,9 +177,9 @@ def tile_gcn_pa_kernel(tc, x, W1_words, W1_scales, out):
         for c in range(2):
             step("SP", "ldw%d" % c, [], lambda c=c: load_w(c))
 
-        def transpose_x(i, k):
+        def transpose_x(i):
             x_words = x_rows[i][:].bitcast(F32)
-            xt = new_bank("tx%d" % i, k)
+            xt = new_bank("tx%d" % i)
             for g in range(PASSES):
                 for u in range(2):
                     plane = 2 * g + u
@@ -111,11 +189,12 @@ def tile_gcn_pa_kernel(tc, x, W1_words, W1_scales, out):
                         identity[:],
                     )
 
-        def group_x(i):
-            nc.scalar.copy(
-                out=grouped[i][:].bitcast(F32),
-                in_=bank_of["tx%d" % i][:].rearrange("p (g u r) -> p g r u", g=PASSES, u=2),
-            )
+        def group_x(i, engine):
+            source = bank_of["tx%d" % i][:].rearrange("p (g u r) -> p g r u", g=PASSES, u=2)
+            if engine == "S":
+                nc.scalar.copy(out=grouped[i][:].bitcast(F32), in_=source)
+            else:
+                nc.vector.tensor_copy(out=grouped[i][:].bitcast(F32), in_=source)
 
         def quantise_x(i):
             for g in range(PASSES):
@@ -126,12 +205,13 @@ def tile_gcn_pa_kernel(tc, x, W1_words, W1_scales, out):
                 )
 
         for i in range(TILES):
-            k, former = claim_bank("tx%d" % i, ["ex%d" % i])
-            step("PE", "tx%d" % i, ["ldx%d" % i] + former, lambda i=i, k=k: transpose_x(i, k))
-            step("S", "ex%d" % i, ["tx%d" % i], lambda i=i: group_x(i))
+            engine = "V" if i in X_LEAVES_BY_VECTOR else "S"
+            step("PE", "tx%d" % i, ["ldx%d" % i], lambda i=i: transpose_x(i), readers=["ex%d" % i])
+            step(engine, "ex%d" % i, ["tx%d" % i], lambda i=i, engine=engine: group_x(i, engine))
             step("V", "qx%d" % i, ["ex%d" % i], lambda i=i: quantise_x(i))
 
-        def product(bank, stat_codes, stat_scales, stat_block, move_codes, move_scales, c0, c1):
+        def product(name, stat_codes, stat_scales, stat_block, move_codes, move_scales, c0, c1):
+            bank = new_bank(name)
             widths = {1: [1], 2: [2], 3: [2, 1], 4: [4]}[c1 - c0]
             start = 0
             for width in widths:
@@ -147,135 +227,124 @@ def tile_gcn_pa_kernel(tc, x, W1_words, W1_scales, out):
                     )
                 start += width
 
-        ht_sb = {}
-
-        def products(u, i, c0, c1, k_ht, k_h):
-            product(new_bank("ht" + u, k_ht), w_codes, w_scales, i, x_codes, x_scales, c0, c1)
-            product(new_bank("h" + u, k_h), x_codes, x_scales, i, w_codes, w_scales, c0, c1)
-
         def leave_psum(u, engine, width):
             if engine == "S":
-                nc.scalar.copy(out=ht_sb[u][:, : width * P], in_=bank_of["ht" + u][:, : width * P])
+                nc.scalar.copy(out=ht_sb[u][:, : width * P], in_=bank_of["pt" + u][:, : width * P])
             else:
-                nc.vector.tensor_copy(out=ht_sb[u][:, : width * P], in_=bank_of["ht" + u][:, : width * P])
+                nc.vector.tensor_copy(out=ht_sb[u][:, : width * P], in_=bank_of["pt" + u][:, : width * P])
 
         def multiply(u, i, c0, c1):
             nc.vector.tensor_tensor(
-                out=a[i][:, blocks(c0, c1)], in0=bank_of["h" + u][:, : (c1 - c0) * P], in1=ht_sb[u][:, : (c1 - c0) * P], op=MULT
+                out=a[i][:, blocks(c0, c1)], in0=bank_of["ph" + u][:, : (c1 - c0) * P], in1=ht_sb[u][:, : (c1 - c0) * P], op=MULT
             )
 
         def square(i, c0, c1, source, slot):
             nc.scalar.activation(out=sq[i][:, blocks(c0, c1)], in_=source, func=SQUARE, accum_out=sums[i][:, slot : slot + 1])
 
-        def transposes(key, j, i0, i1, k):
-            at = new_bank(key, k)
+        def transposes(name, j, i0, i1, squared):
+            at = new_bank(name)
             for i in range(i0, i1):
-                nc.tensor.transpose(at[:, blocks(i - i0, i - i0 + 1)], a[i][:, blocks(j, j + 1)], identity[:])
+                source = sq[i] if squared else a[i]
+                nc.tensor.transpose(at[:, blocks(i - i0, i - i0 + 1)], source[:, blocks(j, j + 1)], identity[:])
 
-        def reciprocal(i, slots):
+        def copy_squares(j, i0, i1, source, slot):
+            nc.vector.tensor_scalar(
+                out=sq[j][:, blocks(i0, i1)], in0=source, scalar1=1.0, scalar2=0.0, op0=MULT, op1=ADD, accum_out=sums[j][:, slot : slot + 1]
+            )
+
+        def add_sums(i, slots):
             nc.vector.tensor_reduce(out=total[i][:], in_=sums[i][:, :slots], axis=AXIS_X, op=ADD)
+
+        def reciprocal(i):
             nc.vector.reciprocal(out=inv[i][:], in_=total[i][:])
 
-        def scale(i, engine):
+        def scale(i, engine, c0, c1):
+            part = sq[i][:, blocks(c0, c1)]
             if engine == "V":
-                nc.vector.tensor_scalar(out=sq[i][:], in0=sq[i][:], scalar1=inv[i][:, 0:1], scalar2=None, op0=MULT)
+                nc.vector.tensor_scalar(out=part, in0=part, scalar1=inv[i][:, 0:1], scalar2=None, op0=MULT)
+            elif engine == "S":
+                nc.scalar.activation(out=part, in_=part, func=COPY, scale=inv[i][:, 0:1])
             else:
-                nc.gpsimd.tensor_scalar(out=sq[i][:], in0=sq[i][:], scalar1=inv[i][:, 0:1], scalar2=0.0, op0=MULT, op1=ADD)
+                nc.gpsimd.tensor_scalar(out=part, in0=part, scalar1=inv[i][:, 0:1], scalar2=0.0, op0=MULT, op1=ADD)
 
-        def store(i):
-            nc.sync.dma_start(out=out[blocks(i, i + 1), :], in_=sq[i][:])
+        def store(i, c0, c1):
+            nc.sync.dma_start(out=out[blocks(i, i + 1), blocks(c0, c1)], in_=sq[i][:, blocks(c0, c1)])
 
-        def left(i):
-            return "%d_%d" % (i, i)
+        def unit(i, c0):
+            return "%d_%d" % (i, c0)
 
-        def right(i):
-            return "%d_%d" % (i, max(i, HALF))
+        def units_of(i):
+            return ([(i, i, HALF)] if i < HALF else []) + [(i, max(i, HALF), TILES)]
 
-        def unit_of(i, j):
-            return left(i) if j < HALF else right(i)
+        def unit_with(i, j):
+            return unit(i, i) if j < HALF else unit(i, max(i, HALF))
 
         row_parts = [[] for i in range(TILES)]
+        square_of = {}
 
-        def plan_products(i, c0, c1):
-            u = "%d_%d" % (i, c0)
-            ht_sb[u] = keep.tile([P, BANK], F32, name="ht_sb%d_%d" % (i, c0))
-            k_ht, former_ht = claim_bank("ht" + u, ["e" + u])
-            k_h, former_h = claim_bank("h" + u, ["m" + u])
-            needs = ["lds3", "ldw%d" % (i // HALF), "ldw%d" % (c0 // HALF), "qx%d" % i] + ["qx%d" % j for j in range(c0, c1)]
-            step("PE", "p" + u, needs + former_ht + former_h, lambda: products(u, i, c0, c1, k_ht, k_h))
+        def define_unit(i, c0, c1):
+            u = unit(i, c0)
+            ht_sb[u] = keep.tile([P, BANK], F32, name="ht_sb" + u)
+            engine = "S" if u in LEAVES_BY_SCALAR else "V"
+            step("PE", "pt" + u, ["lds3", "ldw%d" % (i // HALF)] + ["qx%d" % j for j in range(c0, c1)],
+                 lambda: product("pt" + u, w_codes, w_scales, i, x_codes, x_scales, c0, c1), readers=["e" + u])
+            step("PE", "ph" + u, ["lds3", "ldw%d" % (c0 // HALF), "qx%d" % i],
+                 lambda: product("ph" + u, x_codes, x_scales, i, w_codes, w_scales, c0, c1), readers=["m" + u])
+            step(engine, "e" + u, ["pt" + u], lambda: leave_psum(u, engine, c1 - c0))
+            step("V", "m" + u, ["e" + u, "ph" + u], lambda: multiply(u, i, c0, c1))
 
-        def plan_transposes(j, i0, i1):
-            key = "t%d_%d" % (j, i0)
-            k, former = claim_bank(key, ["x%d_%d" % (j, i0)])
-            step("PE", key, ["m" + unit_of(i, j) for i in range(i0, i1)] + former, lambda: transposes(key, j, i0, i1, k))
-
-        def plan_leave(i, c0, c1, engine):
-            u = "%d_%d" % (i, c0)
-            step(engine, "e" + u, ["p" + u], lambda: leave_psum(u, engine, c1 - c0))
-
-        def plan_multiply(i, c0, c1):
-            u = "%d_%d" % (i, c0)
-            step("V", "m" + u, ["e" + u, "p" + u], lambda: multiply(u, i, c0, c1))
-
-        def plan_square(i, c0, c1):
-            u = "%d_%d" % (i, c0)
+        def define_square(i, c0, c1, needs):
+            name = "q" + unit(i, c0)
             slot = len(row_parts[i])
-            row_parts[i].append("q" + u)
-            step("S", "q" + u, ["m" + u], lambda: square(i, c0, c1, a[i][:, blocks(c0, c1)], slot))
+            row_parts[i].append(name)
+            step("S", name, needs, lambda: square(i, c0, c1, a[i][:, blocks(c0, c1)], slot))
+            for need in needs:
+                square_of[need[1:]] = name
 
-        def plan_square_transposed(j, i0, i1):
-            key = "%d_%d" % (j, i0)
+        def define_transposed(j, i0, i1):
+            key = unit(j, i0)
             slot = len(row_parts[j])
             row_parts[j].append("x" + key)
-            step("S", "x" + key, ["t" + key], lambda: square(j, i0, i1, bank_of["t" + key][:, : (i1 - i0) * P], slot))
+            if key in SQUARES_TRANSPOSED:
+                step("PE", "t" + key, [square_of[unit_with(i, j)] for i in range(i0, i1)], lambda: transposes("t" + key, j, i0, i1, True), readers=["x" + key])
+                step("V", "x" + key, ["t" + key], lambda: copy_squares(j, i0, i1, bank_of["t" + key][:, : (i1 - i0) * P], slot))
+            else:
+                step("PE", "t" + key, ["m" + unit_with(i, j) for i in range(i0, i1)], lambda: transposes("t" + key, j, i0, i1, False), readers=["x" + key])
+                step("S", "x" + key, ["t" + key], lambda: square(j, i0, i1, bank_of["t" + key][:, : (i1 - i0) * P], slot))
 
-        def plan_normalise(i):
-            engine = "G" if i < SCALED_BY_GPSIMD else "V"
+        def define_normalise(i):
             slots = len(row_parts[i])
-            step("V", "r%d" % i, row_parts[i], lambda: reciprocal(i, slots))
-            step(engine, "n%d" % i, ["r%d" % i], lambda: scale(i, engine))
-            step("SP", "st%d" % i, ["n%d" % i], lambda: store(i))
+            step("V", "rs%d" % i, row_parts[i], lambda: add_sums(i, slots))
+            step("V", "r%d" % i, ["rs%d" % i], lambda: reciprocal(i))
+            for part, (engine, c0, c1) in enumerate(SCALE_PARTS[i]):
+                step(engine, "n%d_%d" % (i, part), ["r%d" % i], lambda engine=engine, c0=c0, c1=c1: scale(i, engine, c0, c1))
+            for part, (c0, c1, needs) in enumerate(STORE_PARTS[i]):
+                step("SP", "st%d_%d" % (i, part), ["n%d_%d" % (i, n) for n in needs], lambda c0=c0, c1=c1: store(i, c0, c1))
 
-        for i in range(TILES + 1):
-            if i < HALF:
-                plan_products(i, i, HALF)
-            if i < TILES:
-                plan_products(i, max(i, HALF), TILES)
-                if i >= 1:
-                    plan_transposes(i, 0, min(i, HALF))
-                if i > HALF:
-                    plan_transposes(i, HALF, i)
-            if i < HALF:
-                plan_leave(i, i, HALF, "S")
+        for i in range(TILES):
+            for (row, c0, c1) in units_of(i):
+                define_unit(i, c0, c1)
+            if ONE_SQUARE_A_ROW:
+                define_square(i, i, TILES, ["m" + unit(i, c0) for (row, c0, c1) in units_of(i)])
+            else:
+                for (row, c0, c1) in units_of(i):
+                    define_square(i, c0, c1, ["m" + unit(i, c0)])
             if i >= 1:
-                plan_square(i - 1, max(i - 1, HALF), TILES)
-            if 1 <= i < TILES:
-                plan_square_transposed(i, 0, min(i, HALF))
-            if HALF < i < TILES:
-                plan_square_transposed(i, HALF, i)
-            if i < HALF:
-                plan_square(i, i, HALF)
-            if i < HALF:
-                plan_multiply(i, i, HALF)
-            if i < TILES:
-                plan_leave(i, max(i, HALF), TILES, "V")
-                plan_multiply(i, max(i, HALF), TILES)
-            if i >= 1:
-                plan_normalise(i - 1)
+                define_transposed(i, 0, min(i, HALF))
+            if i > HALF:
+                define_transposed(i, HALF, i)
+            define_normalise(i)
 
-        written = set()
-        position = dict((engine, 0) for engine in order)
-        left_to_write = len(steps)
-        while left_to_write > 0:
-            before = left_to_write
-            for engine in order:
-                while position[engine] < len(order[engine]):
-                    name = order[engine][position[engine]]
-                    needs, fn = steps[name]
-                    if not all(need in written for need in needs):
-                        break
-                    fn()
-                    written.add(name)
-                    position[engine] += 1
-                    left_to_write -= 1
-            assert left_to_write < before, "the engines' orders wait for each other"
+        order = make_order(units_of, unit)
+        for engine in order:
+            for name in order[engine]:
+                assert engine_of[name] == engine, name
+        assert sum(len(order[engine]) for engine in order) == len(steps)
+
+        readers_of_bank = {}
+        for count, name in enumerate(order["PE"]):
+            bank_number[name] = count % BANKS
+            steps[name][0].extend(readers_of_bank.get(count % BANKS, []))
+            readers_of_bank[count % BANKS] = fills[name]
+
+        write_in_order(steps, order)

@@ -32,9 +32,15 @@ LEAVES_BY_SCALAR = ("0_0", "1_1", "2_2", "3_3")
 ONE_SQUARE_A_ROW = False
 SCALE_PARTS = [[("G" if i < 5 else "V", 0, TILES)] for i in range(TILES)]
 STORE_PARTS = [[(0, TILES, [0])] for i in range(TILES)]
-LOADS = ["ldx%d" % i for i in range(TILES)] + ["lds%d" % q for q in range(4)] + ["ldw0", "ldw1"]
+W_LOADS = [(0, 4), (4, 8)]
+LOADS = ["ldx%d" % i for i in range(TILES)] + ["lds%d" % q for q in range(4)] + ["ldw%d" % c0 for (c0, c1) in W_LOADS]
 SQUARES_TRANSPOSED = ()
 H_FIRST = ()
+EARLY_LEFT = False
+SQUARED_BY_VECTOR = ()
+S_PLACE = 0
+MULTIPLIED_BY_GPSIMD = ()
+T_STAGE = [0, 1, 2, 3, 4, 5, 6, 7]
 
 
 def make_order(units_of, unit):
@@ -50,45 +56,50 @@ def make_order(units_of, unit):
         for part in range(len(STORE_PARTS[i])):
             order["SP"].append("st%d_%d" % (i, part))
     def by_vector(i):
-        return 0 <= i < TILES and SCALE_PARTS[i][0][0] == "V"
+        return SCALE_PARTS[i][0][0] == "V"
+    def complete_in(stage):
+        return [j for j in range(TILES) if T_STAGE[j] == stage]
     for i in range(TILES + 2):
         left = unit(i, i)
         right = unit(i, max(i, HALF))
         before = unit(i - 1, max(i - 1, HALF))
         if i < HALF:
-            order["PE"] += ["pt" + left, "ph" + left] + (["ph" + right, "pt" + right] if i in H_FIRST else ["pt" + right, "ph" + right])
-        elif i < TILES:
+            order["PE"] += ["pt" + left, "ph" + left]
+        if i < TILES:
             order["PE"] += ["pt" + right, "ph" + right]
-        if 1 <= i < TILES:
-            order["PE"].append("t" + unit(i, 0))
-        if HALF < i < TILES:
-            order["PE"].append("t" + unit(i, HALF))
+        for j in complete_in(i):
+            if j >= 1:
+                order["PE"].append("t" + unit(j, 0))
+            if j > HALF:
+                order["PE"].append("t" + unit(j, HALF))
         if i < HALF:
             order["S"].append("e" + left)
-        if i < TILES and right in LEAVES_BY_SCALAR:
-            order["S"].append("e" + right)
-        if 1 <= i <= TILES:
+        if 1 <= i <= TILES and before not in SQUARED_BY_VECTOR:
             order["S"].append("q" + before)
         if i < HALF:
             order["S"].append("q" + left)
-        if 1 <= i < TILES:
-            order["S"].append("x" + unit(i, 0))
-        if HALF < i < TILES:
-            order["S"].append("x" + unit(i, HALF))
+        for j in complete_in(i):
+            if j >= 1:
+                order["S"].append("x" + unit(j, 0))
+            if j > HALF:
+                order["S"].append("x" + unit(j, HALF))
         if i < HALF:
             order["V"].append("m" + left)
-        if i < TILES and right not in LEAVES_BY_SCALAR:
+        if i < TILES:
             order["V"].append("e" + right)
-        if by_vector(i - 2):
-            scale_and_store(i - 2)
-        if 1 <= i <= TILES:
-            order["V"].append("rs%d" % (i - 1))
+        if 1 <= i <= TILES and before in SQUARED_BY_VECTOR:
+            order["V"].append("q" + before)
+        for j in complete_in(i - 2):
+            if by_vector(j):
+                scale_and_store(j)
+        for j in complete_in(i - 1):
+            order["V"].append("rs%d" % j)
         if i < TILES:
             order["V"].append("m" + right)
-        if 1 <= i <= TILES:
-            order["V"].append("r%d" % (i - 1))
-            if not by_vector(i - 1):
-                scale_and_store(i - 1)
+        for j in complete_in(i - 1):
+            order["V"].append("r%d" % j)
+            if not by_vector(j):
+                scale_and_store(j)
     return order
 
 
@@ -124,7 +135,7 @@ def tile_gcn_pa_kernel(tc, x, W1_words, W1_scales, out):
         x_codes = keep.tile([P, PASSES, N], U32, name="x_codes", align_bytes=64)
         x_scales = keep.tile([P, PASSES, N], U8, name="x_scales", align_bytes=64)
         w_codes = keep.tile([P, PASSES, N], U32, name="w_codes", align_bytes=64)
-        w_scales = keep.tile([P, PASSES, N], U8, name="w_scales", align_bytes=64)
+        w_scales = keep.tile([P, N], U8, name="w_scales", align_bytes=64)
 
         x_rows = [keep.tile([P, D], BF16, name="x_rows%d" % i) for i in range(TILES)]
         grouped = [keep.tile([P, PASSES, P, PACK], BF16, name="grouped%d" % i, align_bytes=64) for i in range(TILES)]
@@ -134,6 +145,7 @@ def tile_gcn_pa_kernel(tc, x, W1_words, W1_scales, out):
         total = [keep.tile([P, 1], F32, name="total%d" % i) for i in range(TILES)]
         inv = [keep.tile([P, 1], F32, name="inv%d" % i) for i in range(TILES)]
         ht_sb = {}
+        h_sb = {}
 
         def blocks(c0, c1):
             return slice(c0 * P, c1 * P)
@@ -159,23 +171,26 @@ def tile_gcn_pa_kernel(tc, x, W1_words, W1_scales, out):
 
         def load_w_scales(quad):
             nc.sync.dma_start(
-                out=w_scales[32 * quad : 32 * quad + 4, :, :].bitcast(I32),
-                in_=W1_scales[:, 4 * quad : 4 * quad + 4, :].rearrange("g r n -> r g n").bitcast(I32),
+                out=w_scales[32 * quad : 32 * quad + 4 * PASSES, :].bitcast(I32),
+                in_=W1_scales[:, 4 * quad : 4 * quad + 4, :].bitcast(I32),
             )
 
-        def load_w(c):
+        def load_w(c0, c1):
             nc.sync.dma_start(
-                out=w_codes[:, :, blocks(HALF * c, HALF * (c + 1))].bitcast(I32),
-                in_=W1_words[:, :, blocks(HALF * c, HALF * (c + 1)), :].rearrange("g p n t -> p g (n t)").bitcast(I32),
+                out=w_codes[:, :, blocks(c0, c1)].bitcast(I32),
+                in_=W1_words[:, :, blocks(c0, c1), :].rearrange("g p n t -> p g (n t)").bitcast(I32),
             )
+
+        def w_loads(c0, c1):
+            return ["ldw%d" % b0 for (b0, b1) in W_LOADS if b0 < c1 and c0 < b1]
 
         step("V", "zero", [], lambda: nc.vector.memset(w_scales[:].bitcast(I32), 0))
         for i in range(TILES):
             step("SP", "ldx%d" % i, [], lambda i=i: load_x(i))
         for quad in range(4):
             step("SP", "lds%d" % quad, ["zero"], lambda quad=quad: load_w_scales(quad))
-        for c in range(2):
-            step("SP", "ldw%d" % c, [], lambda c=c: load_w(c))
+        for (c0, c1) in W_LOADS:
+            step("SP", "ldw%d" % c0, [], lambda c0=c0, c1=c1: load_w(c0, c1))
 
         def transpose_x(i):
             x_words = x_rows[i][:].bitcast(F32)
@@ -210,6 +225,9 @@ def tile_gcn_pa_kernel(tc, x, W1_words, W1_scales, out):
             step(engine, "ex%d" % i, ["tx%d" % i], lambda i=i, engine=engine: group_x(i, engine))
             step("V", "qx%d" % i, ["ex%d" % i], lambda i=i: quantise_x(i))
 
+        def plane(scales, g, cols):
+            return w_scales[4 * g :, cols] if scales is w_scales else scales[:, g, cols]
+
         def product(name, stat_codes, stat_scales, stat_block, move_codes, move_scales, c0, c1):
             bank = new_bank(name)
             widths = {1: [1], 2: [2], 3: [2, 1], 4: [4]}[c1 - c0]
@@ -219,9 +237,9 @@ def tile_gcn_pa_kernel(tc, x, W1_words, W1_scales, out):
                     nc.tensor.matmul_mx(
                         out=bank[:, blocks(start, start + width)],
                         lhsT=stat_codes[:, g, blocks(stat_block, stat_block + 1)].bitcast(FP8X4),
-                        lhsT_scale=stat_scales[:, g, blocks(stat_block, stat_block + 1)],
+                        lhsT_scale=plane(stat_scales, g, blocks(stat_block, stat_block + 1)),
                         rhs=move_codes[:, g, blocks(c0 + start, c0 + start + width)].bitcast(FP8X4),
-                        rhs_scale=move_scales[:, g, blocks(c0 + start, c0 + start + width)],
+                        rhs_scale=plane(move_scales, g, blocks(c0 + start, c0 + start + width)),
                         start=(g == 0),
                         stop=(g == PASSES - 1),
                     )
@@ -286,18 +304,30 @@ def tile_gcn_pa_kernel(tc, x, W1_words, W1_scales, out):
             u = unit(i, c0)
             ht_sb[u] = keep.tile([P, BANK], F32, name="ht_sb" + u)
             engine = "S" if u in LEAVES_BY_SCALAR else "V"
-            step("PE", "pt" + u, ["lds3", "ldw%d" % (i // HALF)] + ["qx%d" % j for j in range(c0, c1)],
+            step("PE", "pt" + u, ["lds3"] + w_loads(i, i + 1) + ["qx%d" % j for j in range(c0, c1)],
                  lambda: product("pt" + u, w_codes, w_scales, i, x_codes, x_scales, c0, c1), readers=["e" + u])
-            step("PE", "ph" + u, ["lds3", "ldw%d" % (c0 // HALF), "qx%d" % i],
+            step("PE", "ph" + u, ["lds3", "qx%d" % i] + w_loads(c0, c1),
                  lambda: product("ph" + u, x_codes, x_scales, i, w_codes, w_scales, c0, c1), readers=["m" + u])
             step(engine, "e" + u, ["pt" + u], lambda: leave_psum(u, engine, c1 - c0))
-            step("V", "m" + u, ["e" + u, "ph" + u], lambda: multiply(u, i, c0, c1))
+            if u in MULTIPLIED_BY_GPSIMD:
+                h_sb[u] = keep.tile([P, BANK], F32, name="h_sb" + u)
+                fills["ph" + u] = ["f" + u]
+                step("S", "f" + u, ["ph" + u], lambda: nc.scalar.copy(out=h_sb[u][:, : (c1 - c0) * P], in_=bank_of["ph" + u][:, : (c1 - c0) * P]))
+                step("G", "m" + u, ["e" + u, "f" + u], lambda: nc.gpsimd.tensor_tensor(
+                    out=a[i][:, blocks(c0, c1)], in0=h_sb[u][:, : (c1 - c0) * P], in1=ht_sb[u][:, : (c1 - c0) * P], op=MULT))
+            else:
+                step("V", "m" + u, ["e" + u, "ph" + u], lambda: multiply(u, i, c0, c1))
 
         def define_square(i, c0, c1, needs):
             name = "q" + unit(i, c0)
             slot = len(row_parts[i])
             row_parts[i].append(name)
-            step("S", name, needs, lambda: square(i, c0, c1, a[i][:, blocks(c0, c1)], slot))
+            if unit(i, c0) in SQUARED_BY_VECTOR:
+                step("V", name, needs, lambda: nc.vector.scalar_tensor_tensor(
+                    out=sq[i][:, blocks(c0, c1)], in0=a[i][:, blocks(c0, c1)], scalar=1.0, in1=a[i][:, blocks(c0, c1)],
+                    op0=MULT, op1=MULT, accum_out=sums[i][:, slot : slot + 1]))
+            else:
+                step("S", name, needs, lambda: square(i, c0, c1, a[i][:, blocks(c0, c1)], slot))
             for need in needs:
                 square_of[need[1:]] = name
 

@@ -32,7 +32,7 @@ LEAVES_BY_SCALAR = ("0_0", "1_1", "2_2", "3_3")
 ONE_SQUARE_A_ROW = False
 SCALE_PARTS = [[("G" if i < 5 else "V", 0, TILES)] for i in range(TILES)]
 STORE_PARTS = [[(0, TILES, [0])] for i in range(TILES)]
-W_LOADS = [(0, 4), (4, 8)]
+W_LOADS = [(0, 2), (2, 4), (4, 8)]
 LOADS = ["ldx%d" % i for i in range(TILES)] + ["lds%d" % q for q in range(4)] + ["ldw%d" % c0 for (c0, c1) in W_LOADS]
 SQUARES_TRANSPOSED = ()
 H_FIRST = ()

@@ -26,80 +26,54 @@ BANKS = 8
 HALF = BANK // P
 
 FLOPS = 2 * N * N * D
-COPY = mybir.ActivationFunctionType.Copy
-X_LEAVES_BY_VECTOR = ()
-LEAVES_BY_SCALAR = ("0_0", "1_1", "2_2", "3_3")
-ONE_SQUARE_A_ROW = False
-SCALE_PARTS = [[("G" if i < 5 else "V", 0, TILES)] for i in range(TILES)]
-STORE_PARTS = [[(0, TILES, [0])] for i in range(TILES)]
 W_LOADS = [(0, 2), (2, 4), (4, 8)]
 LOADS = ["ldx%d" % i for i in range(TILES)] + ["lds%d" % q for q in range(4)] + ["ldw%d" % c0 for (c0, c1) in W_LOADS]
-SQUARES_TRANSPOSED = ()
-H_FIRST = ()
-EARLY_LEFT = False
+COPIED_BY_SCALAR = ("0_0", "1_1", "2_2", "3_3", "7_7")
+SCALED_BY_GPSIMD = (0, 1, 2)
+TRANSPOSED_AFTER = [0, 2, 3, 3, 4, 5, 6, 7]
+LEFT_FIRST = True
 SQUARED_BY_VECTOR = ()
-S_PLACE = 0
-MULTIPLIED_BY_GPSIMD = ()
-T_STAGE = [0, 1, 2, 3, 4, 5, 6, 7]
+LAST_PARTS = [(0, HALF), (HALF, TILES)]
+BY_MATMUL = (7,)
+LAG = {"ld": -100, "zero": -100, "ex": 0, "vx": -2, "qx": 0.5, "e": 0, "m": 1, "q": 3, "x": 0.5, "rs": 0, "r": 1.5, "n": 1, "st": 0}
 
 
-def make_order(units_of, unit):
-    order = {"PE": [], "V": ["zero"], "S": [], "G": [], "SP": []}
-    order["SP"] += LOADS
+def x_steps(kind, i):
+    return ["%s%d%s" % (kind, i, half) for half in (("a", "b") if i in BY_MATMUL else ("",))]
+
+
+def tensor_order(unit):
+    order = [name for i in range(TILES) for name in x_steps("tx", i)]
+    products = []
     for i in range(TILES):
-        order["PE"].append("tx%d" % i)
-        order["V" if i in X_LEAVES_BY_VECTOR else "S"].append("ex%d" % i)
-        order["V"].append("qx%d" % i)
-    def scale_and_store(i):
-        for part, (engine, c0, c1) in enumerate(SCALE_PARTS[i]):
-            order[engine].append("n%d_%d" % (i, part))
-        for part in range(len(STORE_PARTS[i])):
-            order["SP"].append("st%d_%d" % (i, part))
-    def by_vector(i):
-        return SCALE_PARTS[i][0][0] == "V"
-    def complete_in(stage):
-        return [j for j in range(TILES) if T_STAGE[j] == stage]
-    for i in range(TILES + 2):
-        left = unit(i, i)
-        right = unit(i, max(i, HALF))
-        before = unit(i - 1, max(i - 1, HALF))
-        if i < HALF:
-            order["PE"] += ["pt" + left, "ph" + left]
-        if i < TILES:
-            order["PE"] += ["pt" + right, "ph" + right]
-        for j in complete_in(i):
-            if j >= 1:
-                order["PE"].append("t" + unit(j, 0))
-            if j > HALF:
-                order["PE"].append("t" + unit(j, HALF))
-        if i < HALF:
-            order["S"].append("e" + left)
-        if 1 <= i <= TILES and before not in SQUARED_BY_VECTOR:
-            order["S"].append("q" + before)
-        if i < HALF:
-            order["S"].append("q" + left)
-        for j in complete_in(i):
-            if j >= 1:
-                order["S"].append("x" + unit(j, 0))
-            if j > HALF:
-                order["S"].append("x" + unit(j, HALF))
-        if i < HALF:
-            order["V"].append("m" + left)
-        if i < TILES:
-            order["V"].append("e" + right)
-        if 1 <= i <= TILES and before in SQUARED_BY_VECTOR:
-            order["V"].append("q" + before)
-        for j in complete_in(i - 2):
-            if by_vector(j):
-                scale_and_store(j)
-        for j in complete_in(i - 1):
-            order["V"].append("rs%d" % j)
-        if i < TILES:
-            order["V"].append("m" + right)
-        for j in complete_in(i - 1):
-            order["V"].append("r%d" % j)
-            if not by_vector(j):
-                scale_and_store(j)
+        if i < HALF and not (LEFT_FIRST and i >= 1):
+            products.append((unit(i, i), i, False))
+        if LEFT_FIRST and i + 1 < HALF:
+            products.append((unit(i + 1, i + 1), i + 1, False))
+        products.append((unit(i, max(i, HALF)), i, True))
+    for (u, i, last) in products:
+        order += ["pt" + u, "ph" + u]
+        if last:
+            for j in range(1, TILES):
+                if TRANSPOSED_AFTER[j] == i:
+                    order.append("t" + unit(j, 0))
+                    if j > HALF:
+                        order.append("t" + unit(j, HALF))
+    return order
+
+
+def engine_orders(steps, engine_of, kind_of, tensor):
+    due = dict((name, float(place)) for place, name in enumerate(tensor))
+
+    def place(name):
+        if name not in due:
+            due[name] = max([place(need) for need in steps[name][0]] + [0.0]) + LAG[kind_of[name]]
+        return due[name]
+
+    order = {"PE": tensor, "V": [], "S": [], "G": [], "SP": list(LOADS)}
+    for name in sorted(steps, key=place):
+        if name not in order[engine_of[name]]:
+            order[engine_of[name]].append(name)
     return order
 
 
@@ -131,6 +105,8 @@ def tile_gcn_pa_kernel(tc, x, W1_words, W1_scales, out):
 
         identity = keep.tile([P, P], F32, name="identity")
         make_identity(nc, identity[:])
+        identity_bf16 = keep.tile([P, P], BF16, name="identity_bf16")
+        make_identity(nc, identity_bf16[:])
 
         x_codes = keep.tile([P, PASSES, N], U32, name="x_codes", align_bytes=64)
         x_scales = keep.tile([P, PASSES, N], U8, name="x_scales", align_bytes=64)
@@ -152,6 +128,7 @@ def tile_gcn_pa_kernel(tc, x, W1_words, W1_scales, out):
 
         steps = {}
         engine_of = {}
+        kind_of = {}
         fills = {}
         bank_number = {}
         bank_of = {}
@@ -159,6 +136,11 @@ def tile_gcn_pa_kernel(tc, x, W1_words, W1_scales, out):
         def step(engine, name, needs, fn, readers=None):
             steps[name] = (list(needs), fn)
             engine_of[name] = engine
+            kind_of[name] = name.split("0")[0]
+            for digit in "1234567":
+                kind_of[name] = kind_of[name].split(digit)[0]
+            if kind_of[name] in ("ldx", "lds", "ldw"):
+                kind_of[name] = "ld"
             if readers is not None:
                 fills[name] = readers
 
@@ -204,15 +186,31 @@ def tile_gcn_pa_kernel(tc, x, W1_words, W1_scales, out):
                         identity[:],
                     )
 
-        def group_x(i, engine):
-            source = bank_of["tx%d" % i][:].rearrange("p (g u r) -> p g r u", g=PASSES, u=2)
-            if engine == "S":
-                nc.scalar.copy(out=grouped[i][:].bitcast(F32), in_=source)
-            else:
-                nc.vector.tensor_copy(out=grouped[i][:].bitcast(F32), in_=source)
+        def multiply_x(i, g):
+            name = x_steps("tx", i)[g]
+            xt = new_bank(name)[:].bitcast(BF16)
+            for t in range(PACK):
+                nc.tensor.matmul(
+                    xt[:, t * P : (t + 1) * P],
+                    lhsT=x_rows[i][:, K_PASS * g + t : K_PASS * (g + 1) : PACK],
+                    rhs=identity_bf16[:],
+                    start=True,
+                    stop=True,
+                )
 
-        def quantise_x(i):
-            for g in range(PASSES):
+        def group_x(i):
+            source = bank_of["tx%d" % i][:].rearrange("p (g u r) -> p g r u", g=PASSES, u=2)
+            nc.scalar.copy(out=grouped[i][:].bitcast(F32), in_=source)
+
+        def group_half(i, g):
+            source = bank_of[x_steps("tx", i)[g]][:].bitcast(BF16)[:, : PACK * P].rearrange("p (t r) -> p r t", t=PACK)
+            if g == 0:
+                nc.scalar.copy(out=grouped[i][:, g, :, :], in_=source)
+            else:
+                nc.vector.tensor_copy(out=grouped[i][:, g, :, :], in_=source)
+
+        def quantise_x(i, passes):
+            for g in passes:
                 nc.vector.quantize_mx(
                     out=x_codes[:, g, blocks(i, i + 1)].bitcast(FP8X4),
                     scales=x_scales[:, g, blocks(i, i + 1)],
@@ -220,10 +218,16 @@ def tile_gcn_pa_kernel(tc, x, W1_words, W1_scales, out):
                 )
 
         for i in range(TILES):
-            engine = "V" if i in X_LEAVES_BY_VECTOR else "S"
-            step("PE", "tx%d" % i, ["ldx%d" % i], lambda i=i: transpose_x(i), readers=["ex%d" % i])
-            step(engine, "ex%d" % i, ["tx%d" % i], lambda i=i, engine=engine: group_x(i, engine))
-            step("V", "qx%d" % i, ["ex%d" % i], lambda i=i: quantise_x(i))
+            if i not in BY_MATMUL:
+                step("PE", "tx%d" % i, ["ldx%d" % i], lambda i=i: transpose_x(i), readers=["ex%d" % i])
+                step("S", "ex%d" % i, ["tx%d" % i], lambda i=i: group_x(i))
+                step("V", "qx%d" % i, ["ex%d" % i], lambda i=i: quantise_x(i, range(PASSES)))
+                continue
+            for g in range(PASSES):
+                tx, ex, qx = x_steps("tx", i)[g], x_steps(("ex", "vx")[g], i)[g], x_steps("qx", i)[g]
+                step("PE", tx, ["ldx%d" % i], lambda i=i, g=g: multiply_x(i, g), readers=[ex])
+                step("SV"[g], ex, [tx], lambda i=i, g=g: group_half(i, g))
+                step("V", qx, [ex], lambda i=i, g=g: quantise_x(i, [g]))
 
         def plane(scales, g, cols):
             return w_scales[4 * g :, cols] if scales is w_scales else scales[:, g, cols]
@@ -259,16 +263,10 @@ def tile_gcn_pa_kernel(tc, x, W1_words, W1_scales, out):
         def square(i, c0, c1, source, slot):
             nc.scalar.activation(out=sq[i][:, blocks(c0, c1)], in_=source, func=SQUARE, accum_out=sums[i][:, slot : slot + 1])
 
-        def transposes(name, j, i0, i1, squared):
+        def transposes(name, j, i0, i1):
             at = new_bank(name)
             for i in range(i0, i1):
-                source = sq[i] if squared else a[i]
-                nc.tensor.transpose(at[:, blocks(i - i0, i - i0 + 1)], source[:, blocks(j, j + 1)], identity[:])
-
-        def copy_squares(j, i0, i1, source, slot):
-            nc.vector.tensor_scalar(
-                out=sq[j][:, blocks(i0, i1)], in0=source, scalar1=1.0, scalar2=0.0, op0=MULT, op1=ADD, accum_out=sums[j][:, slot : slot + 1]
-            )
+                nc.tensor.transpose(at[:, blocks(i - i0, i - i0 + 1)], a[i][:, blocks(j, j + 1)], identity[:])
 
         def add_sums(i, slots):
             nc.vector.tensor_reduce(out=total[i][:], in_=sums[i][:, :slots], axis=AXIS_X, op=ADD)
@@ -280,8 +278,6 @@ def tile_gcn_pa_kernel(tc, x, W1_words, W1_scales, out):
             part = sq[i][:, blocks(c0, c1)]
             if engine == "V":
                 nc.vector.tensor_scalar(out=part, in0=part, scalar1=inv[i][:, 0:1], scalar2=None, op0=MULT)
-            elif engine == "S":
-                nc.scalar.activation(out=part, in_=part, func=COPY, scale=inv[i][:, 0:1])
             else:
                 nc.gpsimd.tensor_scalar(out=part, in0=part, scalar1=inv[i][:, 0:1], scalar2=0.0, op0=MULT, op1=ADD)
 
@@ -298,74 +294,55 @@ def tile_gcn_pa_kernel(tc, x, W1_words, W1_scales, out):
             return unit(i, i) if j < HALF else unit(i, max(i, HALF))
 
         row_parts = [[] for i in range(TILES)]
-        square_of = {}
 
         def define_unit(i, c0, c1):
             u = unit(i, c0)
             ht_sb[u] = keep.tile([P, BANK], F32, name="ht_sb" + u)
-            engine = "S" if u in LEAVES_BY_SCALAR else "V"
-            step("PE", "pt" + u, ["lds3"] + w_loads(i, i + 1) + ["qx%d" % j for j in range(c0, c1)],
+            engine = "S" if u in COPIED_BY_SCALAR else "V"
+            step("PE", "pt" + u, ["lds3"] + w_loads(i, i + 1) + [name for j in range(c0, c1) for name in x_steps("qx", j)],
                  lambda: product("pt" + u, w_codes, w_scales, i, x_codes, x_scales, c0, c1), readers=["e" + u])
-            step("PE", "ph" + u, ["lds3", "qx%d" % i] + w_loads(c0, c1),
+            step("PE", "ph" + u, ["lds3"] + x_steps("qx", i) + w_loads(c0, c1),
                  lambda: product("ph" + u, x_codes, x_scales, i, w_codes, w_scales, c0, c1), readers=["m" + u])
             step(engine, "e" + u, ["pt" + u], lambda: leave_psum(u, engine, c1 - c0))
-            if u in MULTIPLIED_BY_GPSIMD:
-                h_sb[u] = keep.tile([P, BANK], F32, name="h_sb" + u)
-                fills["ph" + u] = ["f" + u]
-                step("S", "f" + u, ["ph" + u], lambda: nc.scalar.copy(out=h_sb[u][:, : (c1 - c0) * P], in_=bank_of["ph" + u][:, : (c1 - c0) * P]))
-                step("G", "m" + u, ["e" + u, "f" + u], lambda: nc.gpsimd.tensor_tensor(
-                    out=a[i][:, blocks(c0, c1)], in0=h_sb[u][:, : (c1 - c0) * P], in1=ht_sb[u][:, : (c1 - c0) * P], op=MULT))
-            else:
-                step("V", "m" + u, ["e" + u, "ph" + u], lambda: multiply(u, i, c0, c1))
+            step("V", "m" + u, ["e" + u, "ph" + u], lambda: multiply(u, i, c0, c1))
 
-        def define_square(i, c0, c1, needs):
-            name = "q" + unit(i, c0)
+        def define_square(i, c0, c1):
             slot = len(row_parts[i])
-            row_parts[i].append(name)
+            row_parts[i].append("q" + unit(i, c0))
             if unit(i, c0) in SQUARED_BY_VECTOR:
-                step("V", name, needs, lambda: nc.vector.scalar_tensor_tensor(
+                step("V", "q" + unit(i, c0), ["m" + unit(i, c0)], lambda: nc.vector.scalar_tensor_tensor(
                     out=sq[i][:, blocks(c0, c1)], in0=a[i][:, blocks(c0, c1)], scalar=1.0, in1=a[i][:, blocks(c0, c1)],
                     op0=MULT, op1=MULT, accum_out=sums[i][:, slot : slot + 1]))
             else:
-                step("S", name, needs, lambda: square(i, c0, c1, a[i][:, blocks(c0, c1)], slot))
-            for need in needs:
-                square_of[need[1:]] = name
+                step("S", "q" + unit(i, c0), ["m" + unit(i, c0)], lambda: square(i, c0, c1, a[i][:, blocks(c0, c1)], slot))
 
         def define_transposed(j, i0, i1):
             key = unit(j, i0)
             slot = len(row_parts[j])
             row_parts[j].append("x" + key)
-            if key in SQUARES_TRANSPOSED:
-                step("PE", "t" + key, [square_of[unit_with(i, j)] for i in range(i0, i1)], lambda: transposes("t" + key, j, i0, i1, True), readers=["x" + key])
-                step("V", "x" + key, ["t" + key], lambda: copy_squares(j, i0, i1, bank_of["t" + key][:, : (i1 - i0) * P], slot))
-            else:
-                step("PE", "t" + key, ["m" + unit_with(i, j) for i in range(i0, i1)], lambda: transposes("t" + key, j, i0, i1, False), readers=["x" + key])
-                step("S", "x" + key, ["t" + key], lambda: square(j, i0, i1, bank_of["t" + key][:, : (i1 - i0) * P], slot))
+            step("PE", "t" + key, ["m" + unit_with(i, j) for i in range(i0, i1)], lambda: transposes("t" + key, j, i0, i1), readers=["x" + key])
+            step("S", "x" + key, ["t" + key], lambda: square(j, i0, i1, bank_of["t" + key][:, : (i1 - i0) * P], slot))
 
         def define_normalise(i):
             slots = len(row_parts[i])
+            engine = "G" if i in SCALED_BY_GPSIMD else "V"
             step("V", "rs%d" % i, row_parts[i], lambda: add_sums(i, slots))
             step("V", "r%d" % i, ["rs%d" % i], lambda: reciprocal(i))
-            for part, (engine, c0, c1) in enumerate(SCALE_PARTS[i]):
-                step(engine, "n%d_%d" % (i, part), ["r%d" % i], lambda engine=engine, c0=c0, c1=c1: scale(i, engine, c0, c1))
-            for part, (c0, c1, needs) in enumerate(STORE_PARTS[i]):
-                step("SP", "st%d_%d" % (i, part), ["n%d_%d" % (i, n) for n in needs], lambda c0=c0, c1=c1: store(i, c0, c1))
+            for c0, c1 in LAST_PARTS if i == TILES - 1 else [(0, TILES)]:
+                step(engine, "n%d_%d" % (i, c0), ["r%d" % i], lambda c0=c0, c1=c1: scale(i, engine, c0, c1))
+                step("SP", "st%d_%d" % (i, c0), ["n%d_%d" % (i, c0)], lambda c0=c0, c1=c1: store(i, c0, c1))
 
         for i in range(TILES):
             for (row, c0, c1) in units_of(i):
                 define_unit(i, c0, c1)
-            if ONE_SQUARE_A_ROW:
-                define_square(i, i, TILES, ["m" + unit(i, c0) for (row, c0, c1) in units_of(i)])
-            else:
-                for (row, c0, c1) in units_of(i):
-                    define_square(i, c0, c1, ["m" + unit(i, c0)])
+                define_square(i, c0, c1)
             if i >= 1:
                 define_transposed(i, 0, min(i, HALF))
             if i > HALF:
                 define_transposed(i, HALF, i)
             define_normalise(i)
 
-        order = make_order(units_of, unit)
+        order = engine_orders(steps, engine_of, kind_of, tensor_order(unit))
         for engine in order:
             for name in order[engine]:
                 assert engine_of[name] == engine, name

from contextlib import ExitStack

import concourse.mybir as mybir
from concourse.masks import make_identity

F32 = mybir.dt.float32
BF16 = mybir.dt.bfloat16
I32 = mybir.dt.int32
U32 = mybir.dt.uint32
U8 = mybir.dt.uint8
FP8X4 = mybir.dt.float8_e4m3fn_x4
SQUARE = mybir.ActivationFunctionType.Square
MULT = mybir.AluOpType.mult
ADD = mybir.AluOpType.add
AXIS_X = mybir.AxisListType.X

P = 128
PACK = 4
K_PASS = P * PACK
N = 1024
D = 1024
PASSES = D // K_PASS
TILES = N // P
BANK = 512
BANKS = 8
HALF = BANK // P

FLOPS = 2 * N * N * D
W_LOADS = [(0, 2), (2, 4), (4, 8)]
LOADS = ["ldx%d" % i for i in range(TILES)] + ["lds%d" % q for q in range(4)] + ["ldw%d" % c0 for (c0, c1) in W_LOADS]
COPIED_BY_SCALAR = ("0_0", "1_1", "2_2", "3_3", "7_7")
SCALED_BY_GPSIMD = (0, 1, 2)
TRANSPOSED_AFTER = [0, 2, 3, 3, 4, 5, 6, 7]
LEFT_FIRST = True
SQUARED_BY_VECTOR = ()
LAST_PARTS = [(0, HALF), (HALF, TILES)]
BY_MATMUL = (7,)
LAG = {"ld": -100, "zero": -100, "ex": 0, "vx": -2, "qx": 0.5, "e": 0, "m": 1, "q": 3, "x": 0.5, "rs": 0, "r": 1.5, "n": 1, "st": 0}


def x_steps(kind, i):
    return ["%s%d%s" % (kind, i, half) for half in (("a", "b") if i in BY_MATMUL else ("",))]


def tensor_order(unit):
    order = [name for i in range(TILES) for name in x_steps("tx", i)]
    products = []
    for i in range(TILES):
        if i < HALF and not (LEFT_FIRST and i >= 1):
            products.append((unit(i, i), i, False))
        if LEFT_FIRST and i + 1 < HALF:
            products.append((unit(i + 1, i + 1), i + 1, False))
        products.append((unit(i, max(i, HALF)), i, True))
    for (u, i, last) in products:
        order += ["pt" + u, "ph" + u]
        if last:
            for j in range(1, TILES):
                if TRANSPOSED_AFTER[j] == i:
                    order.append("t" + unit(j, 0))
                    if j > HALF:
                        order.append("t" + unit(j, HALF))
    return order


def engine_orders(steps, engine_of, kind_of, tensor):
    due = dict((name, float(place)) for place, name in enumerate(tensor))

    def place(name):
        if name not in due:
            due[name] = max([place(need) for need in steps[name][0]] + [0.0]) + LAG[kind_of[name]]
        return due[name]

    order = {"PE": tensor, "V": [], "S": [], "G": [], "SP": list(LOADS)}
    for name in sorted(steps, key=place):
        if name not in order[engine_of[name]]:
            order[engine_of[name]].append(name)
    return order


def write_in_order(steps, order):
    written = set()
    position = dict((engine, 0) for engine in order)
    left_to_write = len(steps)
    while left_to_write > 0:
        before = left_to_write
        for engine in order:
            while position[engine] < len(order[engine]):
                name = order[engine][position[engine]]
                needs, fn = steps[name]
                if not all(need in written for need in needs):
                    break
                fn()
                written.add(name)
                position[engine] += 1
                left_to_write -= 1
        assert left_to_write < before, "the engines' orders wait for each other"


def tile_gcn_pa_kernel(tc, x, W1_words, W1_scales, out):
    nc = tc.nc
    with ExitStack() as ctx:
        keep = ctx.enter_context(tc.tile_pool(name="keep", bufs=1))
        psum = ctx.enter_context(tc.psum_pool(name="psum", bufs=1))
        ctx.enter_context(tc.manual_schedule())

        identity = keep.tile([P, P], F32, name="identity")
        make_identity(nc, identity[:])
        identity_bf16 = keep.tile([P, P], BF16, name="identity_bf16")
        make_identity(nc, identity_bf16[:])

        x_codes = keep.tile([P, PASSES, N], U32, name="x_codes", align_bytes=64)
        x_scales = keep.tile([P, PASSES, N], U8, name="x_scales", align_bytes=64)
        w_codes = keep.tile([P, PASSES, N], U32, name="w_codes", align_bytes=64)
        w_scales = keep.tile([P, N], U8, name="w_scales", align_bytes=64)

        x_rows = [keep.tile([P, D], BF16, name="x_rows%d" % i) for i in range(TILES)]
        grouped = [keep.tile([P, PASSES, P, PACK], BF16, name="grouped%d" % i, align_bytes=64) for i in range(TILES)]
        a = [keep.tile([P, N], F32, name="a%d" % i) for i in range(TILES)]
        sq = [keep.tile([P, N], F32, name="sq%d" % i) for i in range(TILES)]
        sums = [keep.tile([P, 4], F32, name="sums%d" % i) for i in range(TILES)]
        total = [keep.tile([P, 1], F32, name="total%d" % i) for i in range(TILES)]
        inv = [keep.tile([P, 1], F32, name="inv%d" % i) for i in range(TILES)]
        ht_sb = {}
        h_sb = {}

        def blocks(c0, c1):
            return slice(c0 * P, c1 * P)

        steps = {}
        engine_of = {}
        kind_of = {}
        fills = {}
        bank_number = {}
        bank_of = {}

        def step(engine, name, needs, fn, readers=None):
            steps[name] = (list(needs), fn)
            engine_of[name] = engine
            kind_of[name] = name.split("0")[0]
            for digit in "1234567":
                kind_of[name] = kind_of[name].split(digit)[0]
            if kind_of[name] in ("ldx", "lds", "ldw"):
                kind_of[name] = "ld"
            if readers is not None:
                fills[name] = readers

        def new_bank(name):
            bank_of[name] = psum.tile([P, BANK], F32, name="ps_" + name, tag="bank%d" % bank_number[name])
            return bank_of[name]

        def load_x(i):
            nc.sync.dma_start(out=x_rows[i][:], in_=x[blocks(i, i + 1), :])

        def load_w_scales(quad):
            nc.sync.dma_start(
                out=w_scales[32 * quad : 32 * quad + 4 * PASSES, :].bitcast(I32),
                in_=W1_scales[:, 4 * quad : 4 * quad + 4, :].bitcast(I32),
            )

        def load_w(c0, c1):
            nc.sync.dma_start(
                out=w_codes[:, :, blocks(c0, c1)].bitcast(I32),
                in_=W1_words[:, :, blocks(c0, c1), :].rearrange("g p n t -> p g (n t)").bitcast(I32),
            )

        def w_loads(c0, c1):
            return ["ldw%d" % b0 for (b0, b1) in W_LOADS if b0 < c1 and c0 < b1]

        step("V", "zero", [], lambda: nc.vector.memset(w_scales[:].bitcast(I32), 0))
        for i in range(TILES):
            step("SP", "ldx%d" % i, [], lambda i=i: load_x(i))
        for quad in range(4):
            step("SP", "lds%d" % quad, ["zero"], lambda quad=quad: load_w_scales(quad))
        for (c0, c1) in W_LOADS:
            step("SP", "ldw%d" % c0, [], lambda c0=c0, c1=c1: load_w(c0, c1))

        def transpose_x(i):
            x_words = x_rows[i][:].bitcast(F32)
            xt = new_bank("tx%d" % i)
            for g in range(PASSES):
                for u in range(2):
                    plane = 2 * g + u
                    nc.tensor.transpose(
                        xt[:, plane * P : (plane + 1) * P],
                        x_words[:, 256 * g + u : 256 * (g + 1) : 2],
                        identity[:],
                    )

        def multiply_x(i, g):
            name = x_steps("tx", i)[g]
            xt = new_bank(name)[:].bitcast(BF16)
            for t in range(PACK):
                nc.tensor.matmul(
                    xt[:, t * P : (t + 1) * P],
                    lhsT=x_rows[i][:, K_PASS * g + t : K_PASS * (g + 1) : PACK],
                    rhs=identity_bf16[:],
                    start=True,
                    stop=True,
                )

        def group_x(i):
            source = bank_of["tx%d" % i][:].rearrange("p (g u r) -> p g r u", g=PASSES, u=2)
            nc.scalar.copy(out=grouped[i][:].bitcast(F32), in_=source)

        def group_half(i, g):
            source = bank_of[x_steps("tx", i)[g]][:].bitcast(BF16)[:, : PACK * P].rearrange("p (t r) -> p r t", t=PACK)
            if g == 0:
                nc.scalar.copy(out=grouped[i][:, g, :, :], in_=source)
            else:
                nc.vector.tensor_copy(out=grouped[i][:, g, :, :], in_=source)

        def quantise_x(i, passes):
            for g in passes:
                nc.vector.quantize_mx(
                    out=x_codes[:, g, blocks(i, i + 1)].bitcast(FP8X4),
                    scales=x_scales[:, g, blocks(i, i + 1)],
                    in_=grouped[i][:, g, :, :].rearrange("p r t -> p (r t)"),
                )

        for i in range(TILES):
            if i not in BY_MATMUL:
                step("PE", "tx%d" % i, ["ldx%d" % i], lambda i=i: transpose_x(i), readers=["ex%d" % i])
                step("S", "ex%d" % i, ["tx%d" % i], lambda i=i: group_x(i))
                step("V", "qx%d" % i, ["ex%d" % i], lambda i=i: quantise_x(i, range(PASSES)))
                continue
            for g in range(PASSES):
                tx, ex, qx = x_steps("tx", i)[g], x_steps(("ex", "vx")[g], i)[g], x_steps("qx", i)[g]
                step("PE", tx, ["ldx%d" % i], lambda i=i, g=g: multiply_x(i, g), readers=[ex])
                step("SV"[g], ex, [tx], lambda i=i, g=g: group_half(i, g))
                step("V", qx, [ex], lambda i=i, g=g: quantise_x(i, [g]))

        def plane(scales, g, cols):
            return w_scales[4 * g :, cols] if scales is w_scales else scales[:, g, cols]

        def product(name, stat_codes, stat_scales, stat_block, move_codes, move_scales, c0, c1):
            bank = new_bank(name)
            widths = {1: [1], 2: [2], 3: [2, 1], 4: [4]}[c1 - c0]
            start = 0
            for width in widths:
                for g in range(PASSES):
                    nc.tensor.matmul_mx(
                        out=bank[:, blocks(start, start + width)],
                        lhsT=stat_codes[:, g, blocks(stat_block, stat_block + 1)].bitcast(FP8X4),
                        lhsT_scale=plane(stat_scales, g, blocks(stat_block, stat_block + 1)),
                        rhs=move_codes[:, g, blocks(c0 + start, c0 + start + width)].bitcast(FP8X4),
                        rhs_scale=plane(move_scales, g, blocks(c0 + start, c0 + start + width)),
                        start=(g == 0),
                        stop=(g == PASSES - 1),
                    )
                start += width

        def leave_psum(u, engine, width):
            if engine == "S":
                nc.scalar.copy(out=ht_sb[u][:, : width * P], in_=bank_of["pt" + u][:, : width * P])
            else:
                nc.vector.tensor_copy(out=ht_sb[u][:, : width * P], in_=bank_of["pt" + u][:, : width * P])

        def multiply(u, i, c0, c1):
            nc.vector.tensor_tensor(
                out=a[i][:, blocks(c0, c1)], in0=bank_of["ph" + u][:, : (c1 - c0) * P], in1=ht_sb[u][:, : (c1 - c0) * P], op=MULT
            )

        def square(i, c0, c1, source, slot):
            nc.scalar.activation(out=sq[i][:, blocks(c0, c1)], in_=source, func=SQUARE, accum_out=sums[i][:, slot : slot + 1])

        def transposes(name, j, i0, i1):
            at = new_bank(name)
            for i in range(i0, i1):
                nc.tensor.transpose(at[:, blocks(i - i0, i - i0 + 1)], a[i][:, blocks(j, j + 1)], identity[:])

        def add_sums(i, slots):
            nc.vector.tensor_reduce(out=total[i][:], in_=sums[i][:, :slots], axis=AXIS_X, op=ADD)

        def reciprocal(i):
            nc.vector.reciprocal(out=inv[i][:], in_=total[i][:])

        def scale(i, engine, c0, c1):
            part = sq[i][:, blocks(c0, c1)]
            if engine == "V":
                nc.vector.tensor_scalar(out=part, in0=part, scalar1=inv[i][:, 0:1], scalar2=None, op0=MULT)
            else:
                nc.gpsimd.tensor_scalar(out=part, in0=part, scalar1=inv[i][:, 0:1], scalar2=0.0, op0=MULT, op1=ADD)

        def store(i, c0, c1):
            nc.sync.dma_start(out=out[blocks(i, i + 1), blocks(c0, c1)], in_=sq[i][:, blocks(c0, c1)])

        def unit(i, c0):
            return "%d_%d" % (i, c0)

        def units_of(i):
            return ([(i, i, HALF)] if i < HALF else []) + [(i, max(i, HALF), TILES)]

        def unit_with(i, j):
            return unit(i, i) if j < HALF else unit(i, max(i, HALF))

        row_parts = [[] for i in range(TILES)]

        def define_unit(i, c0, c1):
            u = unit(i, c0)
            ht_sb[u] = keep.tile([P, BANK], F32, name="ht_sb" + u)
            engine = "S" if u in COPIED_BY_SCALAR else "V"
            step("PE", "pt" + u, ["lds3"] + w_loads(i, i + 1) + [name for j in range(c0, c1) for name in x_steps("qx", j)],
                 lambda: product("pt" + u, w_codes, w_scales, i, x_codes, x_scales, c0, c1), readers=["e" + u])
            step("PE", "ph" + u, ["lds3"] + x_steps("qx", i) + w_loads(c0, c1),
                 lambda: product("ph" + u, x_codes, x_scales, i, w_codes, w_scales, c0, c1), readers=["m" + u])
            step(engine, "e" + u, ["pt" + u], lambda: leave_psum(u, engine, c1 - c0))
            step("V", "m" + u, ["e" + u, "ph" + u], lambda: multiply(u, i, c0, c1))

        def define_square(i, c0, c1):
            slot = len(row_parts[i])
            row_parts[i].append("q" + unit(i, c0))
            if unit(i, c0) in SQUARED_BY_VECTOR:
                step("V", "q" + unit(i, c0), ["m" + unit(i, c0)], lambda: nc.vector.scalar_tensor_tensor(
                    out=sq[i][:, blocks(c0, c1)], in0=a[i][:, blocks(c0, c1)], scalar=1.0, in1=a[i][:, blocks(c0, c1)],
                    op0=MULT, op1=MULT, accum_out=sums[i][:, slot : slot + 1]))
            else:
                step("S", "q" + unit(i, c0), ["m" + unit(i, c0)], lambda: square(i, c0, c1, a[i][:, blocks(c0, c1)], slot))

        def define_transposed(j, i0, i1):
            key = unit(j, i0)
            slot = len(row_parts[j])
            row_parts[j].append("x" + key)
            step("PE", "t" + key, ["m" + unit_with(i, j) for i in range(i0, i1)], lambda: transposes("t" + key, j, i0, i1), readers=["x" + key])
            step("S", "x" + key, ["t" + key], lambda: square(j, i0, i1, bank_of["t" + key][:, : (i1 - i0) * P], slot))

        def define_normalise(i):
            slots = len(row_parts[i])
            engine = "G" if i in SCALED_BY_GPSIMD else "V"
            step("V", "rs%d" % i, row_parts[i], lambda: add_sums(i, slots))
            step("V", "r%d" % i, ["rs%d" % i], lambda: reciprocal(i))
            for c0, c1 in LAST_PARTS if i == TILES - 1 else [(0, TILES)]:
                step(engine, "n%d_%d" % (i, c0), ["r%d" % i], lambda c0=c0, c1=c1: scale(i, engine, c0, c1))
                step("SP", "st%d_%d" % (i, c0), ["n%d_%d" % (i, c0)], lambda c0=c0, c1=c1: store(i, c0, c1))

        for i in range(TILES):
            for (row, c0, c1) in units_of(i):
                define_unit(i, c0, c1)
                define_square(i, c0, c1)
            if i >= 1:
                define_transposed(i, 0, min(i, HALF))
            if i > HALF:
                define_transposed(i, HALF, i)
            define_normalise(i)

        order = engine_orders(steps, engine_of, kind_of, tensor_order(unit))
        for engine in order:
            for name in order[engine]:
                assert engine_of[name] == engine, name
        assert sum(len(order[engine]) for engine in order) == len(steps)

        readers_of_bank = {}
        for count, name in enumerate(order["PE"]):
            bank_number[name] = count % BANKS
            steps[name][0].extend(readers_of_bank.get(count % BANKS, []))
            readers_of_bank[count % BANKS] = fills[name]

        write_in_order(steps, order)
